import numpy as np
import ml_dtypes


def mxq(x, axis, fmt="e4m3"):
    dtype, down = {"e4m3": (ml_dtypes.float8_e4m3fn, 7), "e5m2": (ml_dtypes.float8_e5m2, 14)}[fmt]
    v = np.moveaxis(np.asarray(x, np.float32).astype(ml_dtypes.bfloat16).astype(np.float64), axis, -1)
    blocks = v.reshape(v.shape[:-1] + (-1, 32))
    amax = np.abs(blocks).max(-1, keepdims=True)
    byte = np.maximum(np.where(amax > 0, np.frexp(amax)[1] - 1 + 127, 0) - down, 1)
    scale = np.exp2(byte - 127.0)
    codes = (blocks / scale).astype(np.float32).astype(dtype).astype(np.float64)
    return np.moveaxis((codes * scale).reshape(v.shape), -1, axis)


WIDE = False


def mx_kscale(k):
    if not WIDE:
        return np.ones(k)
    levels = np.array([10, -10, 5, -5, 0])
    a = np.random.permutation(np.resize(levels, k // 512 * 4)).reshape(k // 512, 4)
    idx = np.arange(k)
    return np.exp2(a[idx // 512, idx % 128 // 32])


BF16 = ml_dtypes.bfloat16


def bf(x):
    return np.asarray(x, np.float32).astype(BF16)


def f64(x):
    return np.asarray(x).astype(np.float64)


B, SA, SB, D, H, DH = 4, 768, 256, 512, 4, 128
S = SA + SB
EPS = 1e-6


def make_rope(s, dh):
    pos = np.arange(s, dtype=np.float64)
    inv_freq = 1.0 / (10000.0 ** (np.arange(0, dh, 2, dtype=np.float64) / dh))
    theta = pos[:, None] * inv_freq[None, :]
    cos, sin = np.cos(theta), np.sin(theta)
    row0 = np.stack([cos, -sin], axis=-1)
    row1 = np.stack([sin, cos], axis=-1)
    return np.stack([row0, row1], axis=-2)[None, None]


def rms_norm(x, w):
    return x * (1.0 / np.sqrt(np.mean(x * x, axis=-1, keepdims=True) + EPS)) * w


def apply_rope(x, freqs):
    x_ = x.reshape(*x.shape[:-1], -1, 1, 2)
    out = freqs[..., 0] * x_[..., 0] + freqs[..., 1] * x_[..., 1]
    return out.reshape(x.shape)


def qkv(x, w, b):
    y = (mxq(x, 2, "e4m3") @ mxq(w, 1, "e4m3").T) + b
    y = y.reshape(x.shape[0], x.shape[1], 3 * H, DH).transpose(0, 2, 1, 3)
    return y[:, :H], y[:, H:2 * H], y[:, 2 * H:]


def setup_inputs():
    sa, sb = mx_kscale(D), mx_kscale(D)
    return {
        "hidden_states_a": bf(np.random.standard_normal((B, SA, D)) * sa),
        "hidden_states_b": bf(np.random.standard_normal((B, SB, D)) * sb),
        "image_rotary_emb": bf(make_rope(S, DH)),
        "a_qkv_w": bf(np.random.standard_normal((3 * D, D)) / np.sqrt(D) / sa),
        "a_qkv_b": bf(np.random.standard_normal(3 * D) * 0.2),
        "b_qkv_w": bf(np.random.standard_normal((3 * D, D)) / np.sqrt(D) / sb),
        "b_qkv_b": bf(np.random.standard_normal(3 * D) * 0.2),
        "norm_q_a_w": bf(1.5 + 0.15 * np.random.standard_normal(DH)),
        "norm_k_a_w": bf(1.5 + 0.15 * np.random.standard_normal(DH)),
        "norm_q_b_w": bf(1.5 + 0.15 * np.random.standard_normal(DH)),
        "norm_k_b_w": bf(1.5 + 0.15 * np.random.standard_normal(DH)),
    }


def reference(hidden_states_a, hidden_states_b, image_rotary_emb, a_qkv_w, a_qkv_b, b_qkv_w, b_qkv_b,
              norm_q_a_w, norm_k_a_w, norm_q_b_w, norm_k_b_w):
    q_a, k_a, v_a = qkv(f64(hidden_states_a), f64(a_qkv_w), f64(a_qkv_b))
    q_a = rms_norm(q_a, f64(norm_q_a_w))
    k_a = rms_norm(k_a, f64(norm_k_a_w))
    q_b, k_b, v_b = qkv(f64(hidden_states_b), f64(b_qkv_w), f64(b_qkv_b))
    q_b = rms_norm(q_b, f64(norm_q_b_w))
    k_b = rms_norm(k_b, f64(norm_k_b_w))
    q = np.concatenate([q_b, q_a], axis=2)
    k = np.concatenate([k_b, k_a], axis=2)
    v = np.concatenate([v_b, v_a], axis=2)
    f = f64(image_rotary_emb)
    return apply_rope(q, f), apply_rope(k, f), v

@@ -1,0 +1,248 @@
+from contextlib import ExitStack
+
+import concourse.mybir as mybir
+from concourse.masks import make_identity
+
+F32 = mybir.dt.float32
+BF16 = mybir.dt.bfloat16
+U32 = mybir.dt.uint32
+U8 = mybir.dt.uint8
+FP8X4 = mybir.dt.float8_e4m3fn_x4
+ACT = mybir.ActivationFunctionType
+ALU = mybir.AluOpType
+
+P = 128
+BATCH = 4
+HEADS = 4
+DH = 128
+PAIRS = DH // 2
+K = 512
+PACK = 4
+HALVES = 2
+BLOCK = HEADS * DH
+ROWS = 2
+UNIT = P * ROWS
+GROUPS = 1024 // UNIT
+EPS = 1e-6
+
+FLOPS = 2 * BATCH * 1024 * K * 3 * BLOCK
+
+
+def tile_fluxjointattention_pa_t_kernel(
+    tc,
+    hidden_states_a,
+    hidden_states_b,
+    image_rotary_emb,
+    a_qkv_w,
+    a_qkv_b,
+    b_qkv_w,
+    b_qkv_b,
+    norm_q_a_w,
+    norm_k_a_w,
+    norm_q_b_w,
+    norm_k_b_w,
+    out_0,
+    out_1,
+    out_2,
+):
+    nc = tc.nc
+    outs = (out_0, out_1, out_2)
+    hidden = (hidden_states_b, hidden_states_a)
+    weights = (b_qkv_w, a_qkv_w)
+    biases = (b_qkv_b, a_qkv_b)
+    gains = ((norm_q_b_w, norm_k_b_w), (norm_q_a_w, norm_k_a_w))
+
+    with ExitStack() as stack:
+        keep = stack.enter_context(tc.tile_pool(name="keep", bufs=1))
+        stage = stack.enter_context(tc.tile_pool(name="stage", bufs=2))
+        work = stack.enter_context(tc.tile_pool(name="work", bufs=3))
+        turn_psum = stack.enter_context(tc.psum_pool(name="turn_psum", bufs=2))
+        mx_psum = stack.enter_context(tc.psum_pool(name="mx_psum", bufs=6))
+
+        ident = keep.tile([P, P], F32)
+        make_identity(nc, ident[:])
+        to_planes = keep.tile([P, P], F32)
+        nc.vector.tensor_copy(
+            out=to_planes[:].rearrange("p (i j) -> p i j", i=2),
+            in_=ident[:].rearrange("p (j i) -> p i j", i=2),
+        )
+        eps = keep.tile([P, 1], F32)
+        nc.vector.memset(eps[:], EPS)
+        warm = keep.tile([P, 1], F32)
+        nc.scalar.activation(out=warm[:], in_=eps[:], func=ACT.Sqrt)
+
+        x_raw = {}
+        w_raw = {}
+
+        def load_tokens(g, b):
+            s, first = (0, 0) if g == 0 else (1, (g - 1) * UNIT)
+            rows = keep.tile([P, ROWS, K], BF16, name="x_raw_%d_%d" % (g, b))
+            nc.sync.dma_start(
+                out=rows[:], in_=hidden[s][b, first : first + UNIT, :].rearrange("(p r) k -> p r k", r=ROWS)
+            )
+            x_raw[g, b] = rows
+
+        def load_weight_block(s, blk):
+            rows = keep.tile([P, HEADS, K], BF16, name="w_raw_%d_%d" % (s, blk))
+            nc.sync.dma_start(
+                out=rows[:], in_=weights[s][blk * BLOCK : (blk + 1) * BLOCK, :].rearrange("(h p) k -> p h k", p=P)
+            )
+            w_raw[s, blk] = rows
+
+        load_tokens(0, 0)
+        for blk in range(3):
+            load_weight_block(0, blk)
+        rope_raw = keep.tile([P, GROUPS, ROWS, PACK * PAIRS], BF16)
+        nc.sync.dma_start(
+            out=rope_raw[:],
+            in_=image_rotary_emb.rearrange("x y (g p r) j i c -> p (x y g) r (j i c)", g=GROUPS, r=ROWS),
+        )
+        for b in range(1, BATCH):
+            load_tokens(0, b)
+        for blk in range(3):
+            load_weight_block(1, blk)
+        for g in range(1, GROUPS):
+            for b in range(BATCH):
+                load_tokens(g, b)
+
+        bias_raw = keep.tile([P, 2, 3 * BLOCK], BF16)
+        gain_raw = keep.tile([P, 2, 2, DH], BF16)
+        for s in range(2):
+            nc.scalar.dma_start(out=bias_raw[:, s, :], in_=biases[s].partition_broadcast(P))
+            for qk in range(2):
+                nc.scalar.dma_start(out=gain_raw[:, s, qk, :], in_=gains[s][qk].partition_broadcast(P))
+
+        bias = keep.tile([P, 2, 3 * BLOCK], F32)
+        coef = keep.tile([P, GROUPS, ROWS, 2, 2 * DH], F32)
+        w_codes = keep.tile([P, 2, 3 * BLOCK], U32, align_bytes=64)
+        w_scales = keep.tile([P, 2, 3 * BLOCK], U8, align_bytes=64)
+
+        def prepare_tables(s, eng):
+            eng.tensor_copy(
+                out=bias[:, s, 0 : 2 * BLOCK].rearrange("p (m i j) -> p m i j", i=2, j=PAIRS),
+                in_=bias_raw[:, s, 0 : 2 * BLOCK].rearrange("p (m j i) -> p m i j", i=2, j=PAIRS),
+            )
+            eng.tensor_copy(out=bias[:, s, 2 * BLOCK :], in_=bias_raw[:, s, 2 * BLOCK :])
+            for g in range(GROUPS):
+                if (g == 0) != (s == 0):
+                    continue
+                for r in range(ROWS):
+                    for qk in range(2):
+                        eng.tensor_tensor(
+                            out=coef[:, g, r, qk, :].rearrange("p (c i j) -> p c i j", c=2, i=2),
+                            in0=rope_raw[:, g, r, :].rearrange("p (j i c) -> p c i j", i=2, c=2),
+                            in1=gain_raw[:, s, qk, :]
+                            .rearrange("p (j c) -> p c j", c=2)
+                            .unsqueeze(2)
+                            .to_broadcast([P, 2, 2, PAIRS]),
+                            op=ALU.mult,
+                        )
+
+        def turn_and_group(raw_rows, order, words):
+            turned = turn_psum.tile([P, 2, HALVES, P], F32, name="turned")
+            for t in range(2):
+                for u in range(HALVES):
+                    nc.tensor.transpose(turned[:, t, u, :], raw_rows(t)[:, u * P : (u + 1) * P], order[:])
+            nc.scalar.copy(out=words, in_=turned[:].rearrange("p t u n -> p t n u"))
+
+        def quantise_weight_block(s, blk):
+            order = ident if blk == 2 else to_planes
+            grouped = stage.tile([P, BLOCK * PACK], BF16, align_bytes=64, name="w_grouped")
+            words = grouped[:].bitcast(F32).rearrange("p (h n u) -> p h n u", h=HEADS, u=HALVES)
+            for first in range(0, HEADS, 2):
+                turn_and_group(
+                    lambda t: w_raw[s, blk][:, first + t, :].bitcast(F32), order, words[:, first : first + 2]
+                )
+            cols = slice(blk * BLOCK, (blk + 1) * BLOCK)
+            nc.vector.quantize_mx(
+                out=w_codes[:, s, cols].bitcast(FP8X4), scales=w_scales[:, s, cols], in_=grouped[:]
+            )
+
+        def quantise_tokens(g, b):
+            grouped = stage.tile([P, UNIT * PACK], BF16, align_bytes=64, name="x_grouped")
+            words = grouped[:].bitcast(F32).rearrange("p (r n u) -> p r n u", r=ROWS, u=HALVES)
+            turn_and_group(lambda r: x_raw[g, b][:, r, :].bitcast(F32), ident, words)
+            codes = work.tile([P, UNIT], U32, align_bytes=64, name="x_codes")
+            scales = work.tile([P, UNIT], U8, align_bytes=64, name="x_scales")
+            nc.vector.quantize_mx(out=codes[:].bitcast(FP8X4), scales=scales[:], in_=grouped[:])
+            return codes, scales
+
+        for g in range(GROUPS):
+            s = 0 if g == 0 else 1
+            if g < 2:
+                prepare_tables(s, nc.vector if s == 0 else nc.gpsimd)
+                for blk in range(3):
+                    quantise_weight_block(s, blk)
+            for b in range(BATCH):
+                x_codes, x_scales = quantise_tokens(g, b)
+                result = work.tile([P, 3, HEADS, ROWS, DH], F32, name="result")
+                for r in range(ROWS):
+                    tokens = slice(r * P, (r + 1) * P)
+                    banks = []
+                    for blk in range(3):
+                        cols = slice(blk * BLOCK, (blk + 1) * BLOCK)
+                        bank = mx_psum.tile([P, BLOCK], F32, name="bank")
+                        nc.tensor.matmul_mx(
+                            out=bank[:],
+                            lhsT=x_codes[:, tokens].bitcast(FP8X4),
+                            lhsT_scale=x_scales[:, tokens],
+                            rhs=w_codes[:, s, cols].bitcast(FP8X4),
+                            rhs_scale=w_scales[:, s, cols],
+                            start=True,
+                            stop=True,
+                        )
+                        banks.append(bank)
+
+                    y = work.tile([P, 2 * BLOCK], F32, name="y")
+                    for blk in range(2):
+                        cols = slice(blk * BLOCK, (blk + 1) * BLOCK)
+                        nc.vector.tensor_tensor(out=y[:, cols], in0=banks[blk][:], in1=bias[:, s, cols], op=ALU.add)
+                    nc.vector.tensor_tensor(
+                        out=result[:, 2, :, r, :],
+                        in0=banks[2][:].rearrange("p (h d) -> p h d", h=HEADS),
+                        in1=bias[:, s, 2 * BLOCK :].rearrange("p (h d) -> p h d", h=HEADS),
+                        op=ALU.add,
+                    )
+
+                    squares = work.tile([P, 2 * BLOCK], BF16, name="squares")
+                    sumsq = work.tile([P, 2 * HEADS], F32, name="sumsq")
+                    for m in range(2 * HEADS):
+                        head = slice(m * DH, (m + 1) * DH)
+                        nc.scalar.activation(
+                            out=squares[:, head], in_=y[:, head], func=ACT.Square, accum_out=sumsq[:, m : m + 1]
+                        )
+                    rms = work.tile([P, 2 * HEADS], F32, name="rms")
+                    nc.scalar.activation(out=rms[:], in_=sumsq[:], func=ACT.Sqrt, scale=1.0 / DH, bias=eps[:])
+                    rinv = work.tile([P, 2 * HEADS], F32, name="rinv")
+                    nc.vector.reciprocal(out=rinv[:], in_=rms[:])
+
+                    part = work.tile([P, 2, 2 * BLOCK], F32, name="part")
+                    for qk in range(2):
+                        cols = slice(qk * BLOCK, (qk + 1) * BLOCK)
+                        y_planes = y[:, cols].rearrange("p (h c j) -> p h c j", c=2, j=PAIRS)
+                        for c in range(2):
+                            nc.vector.tensor_tensor(
+                                out=part[:, c, cols].rearrange("p (h i j) -> p h i j", i=2, j=PAIRS),
+                                in0=y_planes[:, :, c, :].unsqueeze(2).to_broadcast([P, HEADS, 2, PAIRS]),
+                                in1=coef[:, g, r, qk, c * DH : (c + 1) * DH]
+                                .rearrange("p (i j) -> p i j", i=2)
+                                .unsqueeze(1)
+                                .to_broadcast([P, HEADS, 2, PAIRS]),
+                                op=ALU.mult,
+                            )
+                    rotated = work.tile([P, 2 * BLOCK], F32, name="rotated")
+                    nc.gpsimd.tensor_tensor(out=rotated[:], in0=part[:, 0, :], in1=part[:, 1, :], op=ALU.add)
+
+                    for m in range(2 * HEADS):
+                        nc.scalar.activation(
+                            out=result[:, m // HEADS, m % HEADS, r, :].rearrange("p (j i) -> p j i", i=2),
+                            in_=rotated[:, m * DH : (m + 1) * DH].rearrange("p (i j) -> p j i", i=2),
+                            func=ACT.Copy,
+                            scale=rinv[:, m : m + 1],
+                        )
+
+                for which in range(3):
+                    nc.sync.dma_start(
+                        out=outs[which][b, :, g * UNIT : (g + 1) * UNIT, :].rearrange("h (p r) d -> p h (r d)", r=ROWS),
+                        in_=result[:, which].rearrange("p h r d -> p h (r d)"),
+                    )

@@ -57,7 +57,8 @@ def tile_fluxjointattention_pa_t_kernel(
         stage = stack.enter_context(tc.tile_pool(name="stage", bufs=2))
         work = stack.enter_context(tc.tile_pool(name="work", bufs=3))
         turn_psum = stack.enter_context(tc.psum_pool(name="turn_psum", bufs=2))
-        mx_psum = stack.enter_context(tc.psum_pool(name="mx_psum", bufs=6))
+        mx_psum = stack.enter_context(tc.psum_pool(name="mx_psum", bufs=4))
+        coef_psum = stack.enter_context(tc.psum_pool(name="coef_psum", bufs=1))
 
         ident = keep.tile([P, P], F32)
         make_identity(nc, ident[:])
@@ -173,6 +174,17 @@ def tile_fluxjointattention_pa_t_kernel(
                 prepare_tables(s, nc.vector if s == 0 else nc.gpsimd)
                 for blk in range(3):
                     quantise_weight_block(s, blk)
+            coef_banks = []
+            for r in range(ROWS):
+                coef_bank = coef_psum.tile([P, 2 * 2 * DH], F32, name="coef_bank_%d" % r)
+                nc.tensor.matmul(
+                    out=coef_bank[:],
+                    lhsT=ident[:],
+                    rhs=coef[:, g, r].rearrange("p q n -> p (q n)"),
+                    start=True,
+                    stop=True,
+                )
+                coef_banks.append(coef_bank)
             for b in range(BATCH):
                 x_codes, x_scales = quantise_tokens(g, b)
                 result = work.tile([P, 3, HEADS, ROWS, DH], F32, name="result")
@@ -224,7 +236,7 @@ def tile_fluxjointattention_pa_t_kernel(
                             nc.vector.tensor_tensor(
                                 out=part[:, c, cols].rearrange("p (h i j) -> p h i j", i=2, j=PAIRS),
                                 in0=y_planes[:, :, c, :].unsqueeze(2).to_broadcast([P, HEADS, 2, PAIRS]),
-                                in1=coef[:, g, r, qk, c * DH : (c + 1) * DH]
+                                in1=coef_banks[r][:, (2 * qk + c) * DH : (2 * qk + c + 1) * DH]
                                 .rearrange("p (i j) -> p i j", i=2)
                                 .unsqueeze(1)
                                 .to_broadcast([P, HEADS, 2, PAIRS]),

@@ -20,6 +20,7 @@ K = 512
 PACK = 4
 HALVES = 2
 BLOCK = HEADS * DH
+VECTORS = 3 * HEADS
 ROWS = 2
 UNIT = P * ROWS
 GROUPS = 1024 // UNIT
@@ -57,16 +58,12 @@ def tile_fluxjointattention_pa_t_kernel(
         stage = stack.enter_context(tc.tile_pool(name="stage", bufs=2))
         work = stack.enter_context(tc.tile_pool(name="work", bufs=3))
         turn_psum = stack.enter_context(tc.psum_pool(name="turn_psum", bufs=2))
-        mx_psum = stack.enter_context(tc.psum_pool(name="mx_psum", bufs=4))
-        coef_psum = stack.enter_context(tc.psum_pool(name="coef_psum", bufs=1))
+        qk_psum = stack.enter_context(tc.psum_pool(name="qk_psum", bufs=2))
+        back_psum = stack.enter_context(tc.psum_pool(name="back_psum", bufs=3))
+        v_psum = stack.enter_context(tc.psum_pool(name="v_psum", bufs=1))
 
         ident = keep.tile([P, P], F32)
         make_identity(nc, ident[:])
-        to_planes = keep.tile([P, P], F32)
-        nc.vector.tensor_copy(
-            out=to_planes[:].rearrange("p (i j) -> p i j", i=2),
-            in_=ident[:].rearrange("p (j i) -> p i j", i=2),
-        )
         eps = keep.tile([P, 1], F32)
         nc.vector.memset(eps[:], EPS)
         warm = keep.tile([P, 1], F32)
@@ -106,54 +103,59 @@ def tile_fluxjointattention_pa_t_kernel(
             for b in range(BATCH):
                 load_tokens(g, b)
 
-        bias_raw = keep.tile([P, 2, 3 * BLOCK], BF16)
+        bias_rows = keep.tile([P, P], BF16)
+        nc.vector.memset(bias_rows[:], 0.0)
+        v_bias_raw = keep.tile([P, 2, BLOCK], BF16)
         gain_raw = keep.tile([P, 2, 2, DH], BF16)
         for s in range(2):
-            nc.scalar.dma_start(out=bias_raw[:, s, :], in_=biases[s].partition_broadcast(P))
+            nc.scalar.dma_start(
+                out=bias_rows[s * VECTORS : (s + 1) * VECTORS, :], in_=biases[s].rearrange("(m n) -> m n", n=DH)
+            )
+            nc.scalar.dma_start(out=v_bias_raw[:, s, :], in_=biases[s][2 * BLOCK :].partition_broadcast(P))
             for qk in range(2):
                 nc.scalar.dma_start(out=gain_raw[:, s, qk, :], in_=gains[s][qk].partition_broadcast(P))
 
-        bias = keep.tile([P, 2, 3 * BLOCK], F32)
+        bias_rows_f32 = keep.tile([P, P], F32)
+        nc.vector.tensor_copy(out=bias_rows_f32[:], in_=bias_rows[:])
+        bias_turned = turn_psum.tile([P, P], F32, name="turned")
+        nc.tensor.transpose(bias_turned[:], bias_rows_f32[:], ident[:])
+        bias_cols = keep.tile([P, P], F32)
+        nc.vector.tensor_copy(out=bias_cols[:], in_=bias_turned[:])
+
+        v_bias = keep.tile([P, 2, BLOCK], F32)
         coef = keep.tile([P, GROUPS, ROWS, 2, 2 * DH], F32)
         w_codes = keep.tile([P, 2, 3 * BLOCK], U32, align_bytes=64)
         w_scales = keep.tile([P, 2, 3 * BLOCK], U8, align_bytes=64)
 
         def prepare_tables(s, eng):
-            eng.tensor_copy(
-                out=bias[:, s, 0 : 2 * BLOCK].rearrange("p (m i j) -> p m i j", i=2, j=PAIRS),
-                in_=bias_raw[:, s, 0 : 2 * BLOCK].rearrange("p (m j i) -> p m i j", i=2, j=PAIRS),
-            )
-            eng.tensor_copy(out=bias[:, s, 2 * BLOCK :], in_=bias_raw[:, s, 2 * BLOCK :])
+            eng.tensor_copy(out=v_bias[:, s, :], in_=v_bias_raw[:, s, :])
             for g in range(GROUPS):
                 if (g == 0) != (s == 0):
                     continue
                 for r in range(ROWS):
                     for qk in range(2):
                         eng.tensor_tensor(
-                            out=coef[:, g, r, qk, :].rearrange("p (c i j) -> p c i j", c=2, i=2),
-                            in0=rope_raw[:, g, r, :].rearrange("p (j i c) -> p c i j", i=2, c=2),
+                            out=coef[:, g, r, qk, :].rearrange("p (c j i) -> p c j i", c=2, i=2),
+                            in0=rope_raw[:, g, r, :].rearrange("p (j i c) -> p c j i", i=2, c=2),
                             in1=gain_raw[:, s, qk, :]
                             .rearrange("p (j c) -> p c j", c=2)
-                            .unsqueeze(2)
-                            .to_broadcast([P, 2, 2, PAIRS]),
+                            .unsqueeze(3)
+                            .to_broadcast([P, 2, PAIRS, 2]),
                             op=ALU.mult,
                         )
 
-        def turn_and_group(raw_rows, order, words):
+        def turn_and_group(raw_rows, words):
             turned = turn_psum.tile([P, 2, HALVES, P], F32, name="turned")
             for t in range(2):
                 for u in range(HALVES):
-                    nc.tensor.transpose(turned[:, t, u, :], raw_rows(t)[:, u * P : (u + 1) * P], order[:])
+                    nc.tensor.transpose(turned[:, t, u, :], raw_rows(t)[:, u * P : (u + 1) * P], ident[:])
             nc.scalar.copy(out=words, in_=turned[:].rearrange("p t u n -> p t n u"))
 
         def quantise_weight_block(s, blk):
-            order = ident if blk == 2 else to_planes
             grouped = stage.tile([P, BLOCK * PACK], BF16, align_bytes=64, name="w_grouped")
             words = grouped[:].bitcast(F32).rearrange("p (h n u) -> p h n u", h=HEADS, u=HALVES)
             for first in range(0, HEADS, 2):
-                turn_and_group(
-                    lambda t: w_raw[s, blk][:, first + t, :].bitcast(F32), order, words[:, first : first + 2]
-                )
+                turn_and_group(lambda t: w_raw[s, blk][:, first + t, :].bitcast(F32), words[:, first : first + 2])
             cols = slice(blk * BLOCK, (blk + 1) * BLOCK)
             nc.vector.quantize_mx(
                 out=w_codes[:, s, cols].bitcast(FP8X4), scales=w_scales[:, s, cols], in_=grouped[:]
@@ -162,7 +164,7 @@ def tile_fluxjointattention_pa_t_kernel(
         def quantise_tokens(g, b):
             grouped = stage.tile([P, UNIT * PACK], BF16, align_bytes=64, name="x_grouped")
             words = grouped[:].bitcast(F32).rearrange("p (r n u) -> p r n u", r=ROWS, u=HALVES)
-            turn_and_group(lambda r: x_raw[g, b][:, r, :].bitcast(F32), ident, words)
+            turn_and_group(lambda r: x_raw[g, b][:, r, :].bitcast(F32), words)
             codes = work.tile([P, UNIT], U32, align_bytes=64, name="x_codes")
             scales = work.tile([P, UNIT], U8, align_bytes=64, name="x_scales")
             nc.vector.quantize_mx(out=codes[:].bitcast(FP8X4), scales=scales[:], in_=grouped[:])
@@ -174,84 +176,92 @@ def tile_fluxjointattention_pa_t_kernel(
                 prepare_tables(s, nc.vector if s == 0 else nc.gpsimd)
                 for blk in range(3):
                     quantise_weight_block(s, blk)
-            coef_banks = []
-            for r in range(ROWS):
-                coef_bank = coef_psum.tile([P, 2 * 2 * DH], F32, name="coef_bank_%d" % r)
-                nc.tensor.matmul(
-                    out=coef_bank[:],
-                    lhsT=ident[:],
-                    rhs=coef[:, g, r].rearrange("p q n -> p (q n)"),
-                    start=True,
-                    stop=True,
-                )
-                coef_banks.append(coef_bank)
             for b in range(BATCH):
                 x_codes, x_scales = quantise_tokens(g, b)
                 result = work.tile([P, 3, HEADS, ROWS, DH], F32, name="result")
-                for r in range(ROWS):
-                    tokens = slice(r * P, (r + 1) * P)
-                    banks = []
-                    for blk in range(3):
-                        cols = slice(blk * BLOCK, (blk + 1) * BLOCK)
-                        bank = mx_psum.tile([P, BLOCK], F32, name="bank")
+
+                y_turned = work.tile([P, 2 * HEADS, UNIT], F32, name="y_turned")
+                for first in range(0, 2 * HEADS, 2):
+                    qk_bank = qk_psum.tile([P, 2, UNIT], F32, name="qk_bank")
+                    for t in range(2):
+                        m = first + t
                         nc.tensor.matmul_mx(
-                            out=bank[:],
-                            lhsT=x_codes[:, tokens].bitcast(FP8X4),
-                            lhsT_scale=x_scales[:, tokens],
-                            rhs=w_codes[:, s, cols].bitcast(FP8X4),
-                            rhs_scale=w_scales[:, s, cols],
+                            out=qk_bank[:, t, :],
+                            lhsT=w_codes[:, s, m * DH : (m + 1) * DH].bitcast(FP8X4),
+                            lhsT_scale=w_scales[:, s, m * DH : (m + 1) * DH],
+                            rhs=x_codes[:].bitcast(FP8X4),
+                            rhs_scale=x_scales[:],
                             start=True,
                             stop=True,
                         )
-                        banks.append(bank)
+                    for t in range(2):
+                        m = first + t
+                        nc.scalar.activation(
+                            out=y_turned[:, m, :],
+                            in_=qk_bank[:, t, :],
+                            func=ACT.Identity,
+                            bias=bias_cols[:, s * VECTORS + m : s * VECTORS + m + 1],
+                        )
 
-                    y = work.tile([P, 2 * BLOCK], F32, name="y")
-                    for blk in range(2):
-                        cols = slice(blk * BLOCK, (blk + 1) * BLOCK)
-                        nc.vector.tensor_tensor(out=y[:, cols], in0=banks[blk][:], in1=bias[:, s, cols], op=ALU.add)
+                for r in range(ROWS):
+                    tokens = slice(r * P, (r + 1) * P)
+
+                    v_bank = v_psum.tile([P, BLOCK], F32, name="v_bank")
+                    nc.tensor.matmul_mx(
+                        out=v_bank[:],
+                        lhsT=x_codes[:, tokens].bitcast(FP8X4),
+                        lhsT_scale=x_scales[:, tokens],
+                        rhs=w_codes[:, s, 2 * BLOCK :].bitcast(FP8X4),
+                        rhs_scale=w_scales[:, s, 2 * BLOCK :],
+                        start=True,
+                        stop=True,
+                    )
                     nc.vector.tensor_tensor(
                         out=result[:, 2, :, r, :],
-                        in0=banks[2][:].rearrange("p (h d) -> p h d", h=HEADS),
-                        in1=bias[:, s, 2 * BLOCK :].rearrange("p (h d) -> p h d", h=HEADS),
+                        in0=v_bank[:].rearrange("p (h d) -> p h d", h=HEADS),
+                        in1=v_bias[:, s, :].rearrange("p (h d) -> p h d", h=HEADS),
                         op=ALU.add,
                     )
 
-                    squares = work.tile([P, 2 * BLOCK], BF16, name="squares")
-                    sumsq = work.tile([P, 2 * HEADS], F32, name="sumsq")
-                    for m in range(2 * HEADS):
-                        head = slice(m * DH, (m + 1) * DH)
-                        nc.scalar.activation(
-                            out=squares[:, head], in_=y[:, head], func=ACT.Square, accum_out=sumsq[:, m : m + 1]
-                        )
-                    rms = work.tile([P, 2 * HEADS], F32, name="rms")
-                    nc.scalar.activation(out=rms[:], in_=sumsq[:], func=ACT.Sqrt, scale=1.0 / DH, bias=eps[:])
-                    rinv = work.tile([P, 2 * HEADS], F32, name="rinv")
-                    nc.vector.reciprocal(out=rinv[:], in_=rms[:])
-
                     part = work.tile([P, 2, 2 * BLOCK], F32, name="part")
                     for qk in range(2):
-                        cols = slice(qk * BLOCK, (qk + 1) * BLOCK)
-                        y_planes = y[:, cols].rearrange("p (h c j) -> p h c j", c=2, j=PAIRS)
-                        for c in range(2):
-                            nc.vector.tensor_tensor(
-                                out=part[:, c, cols].rearrange("p (h i j) -> p h i j", i=2, j=PAIRS),
-                                in0=y_planes[:, :, c, :].unsqueeze(2).to_broadcast([P, HEADS, 2, PAIRS]),
-                                in1=coef_banks[r][:, (2 * qk + c) * DH : (2 * qk + c + 1) * DH]
-                                .rearrange("p (i j) -> p i j", i=2)
-                                .unsqueeze(1)
-                                .to_broadcast([P, HEADS, 2, PAIRS]),
-                                op=ALU.mult,
+                        y = back_psum.tile([P, BLOCK], F32, name="y")
+                        for h in range(HEADS):
+                            nc.tensor.transpose(
+                                y[:, h * DH : (h + 1) * DH], y_turned[:, qk * HEADS + h, tokens], ident[:]
                             )
-                    rotated = work.tile([P, 2 * BLOCK], F32, name="rotated")
-                    nc.gpsimd.tensor_tensor(out=rotated[:], in0=part[:, 0, :], in1=part[:, 1, :], op=ALU.add)
 
-                    for m in range(2 * HEADS):
-                        nc.scalar.activation(
-                            out=result[:, m // HEADS, m % HEADS, r, :].rearrange("p (j i) -> p j i", i=2),
-                            in_=rotated[:, m * DH : (m + 1) * DH].rearrange("p (i j) -> p j i", i=2),
-                            func=ACT.Copy,
-                            scale=rinv[:, m : m + 1],
-                        )
+                        squares = work.tile([P, BLOCK], BF16, name="squares")
+                        sumsq = work.tile([P, HEADS], F32, name="sumsq")
+                        for h in range(HEADS):
+                            head = slice(h * DH, (h + 1) * DH)
+                            nc.scalar.activation(
+                                out=squares[:, head], in_=y[:, head], func=ACT.Square, accum_out=sumsq[:, h : h + 1]
+                            )
+                        rms = work.tile([P, HEADS], F32, name="rms")
+                        nc.scalar.activation(out=rms[:], in_=sumsq[:], func=ACT.Sqrt, scale=1.0 / DH, bias=eps[:])
+                        rinv = work.tile([P, HEADS], F32, name="rinv")
+                        nc.vector.reciprocal(out=rinv[:], in_=rms[:])
+
+                        for h in range(HEADS):
+                            head = slice((qk * HEADS + h) * DH, (qk * HEADS + h + 1) * DH)
+                            y_pairs = y[:, h * DH : (h + 1) * DH].rearrange("p (j c) -> p j c", c=2)
+                            for c in range(2):
+                                nc.vector.scalar_tensor_tensor(
+                                    out=part[:, c, head].rearrange("p (j i) -> p j i", i=2),
+                                    in0=y_pairs[:, :, c : c + 1].to_broadcast([P, PAIRS, 2]),
+                                    scalar=rinv[:, h : h + 1],
+                                    in1=coef[:, g, r, qk, c * DH : (c + 1) * DH].rearrange("p (j i) -> p j i", i=2),
+                                    op0=ALU.mult,
+                                    op1=ALU.mult,
+                                )
+
+                    nc.gpsimd.tensor_tensor(
+                        out=result[:, 0:2, :, r, :].rearrange("p w h d -> p (w h) d"),
+                        in0=part[:, 0, :].rearrange("p (m d) -> p m d", d=DH),
+                        in1=part[:, 1, :].rearrange("p (m d) -> p m d", d=DH),
+                        op=ALU.add,
+                    )
 
                 for which in range(3):
                     nc.sync.dma_start(

@@ -67,7 +67,7 @@ def tile_fluxjointattention_pa_t_kernel(
         eps = keep.tile([P, 1], F32)
         nc.vector.memset(eps[:], EPS)
         warm = keep.tile([P, 1], F32)
-        nc.scalar.activation(out=warm[:], in_=eps[:], func=ACT.Sqrt)
+        nc.scalar.activation(out=warm[:], in_=eps[:], func=ACT.Abs_reciprocal_sqrt)
 
         x_raw = {}
         w_raw = {}
@@ -115,13 +115,6 @@ def tile_fluxjointattention_pa_t_kernel(
             for qk in range(2):
                 nc.scalar.dma_start(out=gain_raw[:, s, qk, :], in_=gains[s][qk].partition_broadcast(P))
 
-        bias_rows_f32 = keep.tile([P, P], F32)
-        nc.vector.tensor_copy(out=bias_rows_f32[:], in_=bias_rows[:])
-        bias_turned = turn_psum.tile([P, P], F32, name="turned")
-        nc.tensor.transpose(bias_turned[:], bias_rows_f32[:], ident[:])
-        bias_cols = keep.tile([P, P], F32)
-        nc.vector.tensor_copy(out=bias_cols[:], in_=bias_turned[:])
-
         v_bias = keep.tile([P, 2, BLOCK], F32)
         coef = keep.tile([P, GROUPS, ROWS, 2, 2 * DH], F32)
         w_codes = keep.tile([P, 2, 3 * BLOCK], U32, align_bytes=64)
@@ -135,12 +128,12 @@ def tile_fluxjointattention_pa_t_kernel(
                 for r in range(ROWS):
                     for qk in range(2):
                         eng.tensor_tensor(
-                            out=coef[:, g, r, qk, :].rearrange("p (c j i) -> p c j i", c=2, i=2),
-                            in0=rope_raw[:, g, r, :].rearrange("p (j i c) -> p c j i", i=2, c=2),
+                            out=coef[:, g, r, qk, :].rearrange("p (j c i) -> p j c i", c=2, i=2),
+                            in0=rope_raw[:, g, r, :].rearrange("p (j i c) -> p j c i", i=2, c=2),
                             in1=gain_raw[:, s, qk, :]
-                            .rearrange("p (j c) -> p c j", c=2)
+                            .rearrange("p (j c) -> p j c", c=2)
                             .unsqueeze(3)
-                            .to_broadcast([P, 2, PAIRS, 2]),
+                            .to_broadcast([P, PAIRS, 2, 2]),
                             op=ALU.mult,
                         )
 
@@ -170,12 +163,19 @@ def tile_fluxjointattention_pa_t_kernel(
             nc.vector.quantize_mx(out=codes[:].bitcast(FP8X4), scales=scales[:], in_=grouped[:])
             return codes, scales
 
+        bias_cols = keep.tile([P, P], F32)
         for g in range(GROUPS):
             s = 0 if g == 0 else 1
             if g < 2:
                 prepare_tables(s, nc.vector if s == 0 else nc.gpsimd)
                 for blk in range(3):
                     quantise_weight_block(s, blk)
+            if g == 0:
+                bias_rows_f32 = keep.tile([P, P], F32)
+                nc.vector.tensor_copy(out=bias_rows_f32[:], in_=bias_rows[:])
+                bias_turned = turn_psum.tile([P, P], F32, name="turned")
+                nc.tensor.transpose(bias_turned[:], bias_rows_f32[:], ident[:])
+                nc.vector.tensor_copy(out=bias_cols[:], in_=bias_turned[:])
             for b in range(BATCH):
                 x_codes, x_scales = quantise_tokens(g, b)
                 result = work.tile([P, 3, HEADS, ROWS, DH], F32, name="result")
@@ -223,7 +223,7 @@ def tile_fluxjointattention_pa_t_kernel(
                         op=ALU.add,
                     )
 
-                    part = work.tile([P, 2, 2 * BLOCK], F32, name="part")
+                    part = work.tile([P, 2 * HEADS, 2 * DH], F32, name="part")
                     for qk in range(2):
                         y = back_psum.tile([P, BLOCK], F32, name="y")
                         for h in range(HEADS):
@@ -238,28 +238,26 @@ def tile_fluxjointattention_pa_t_kernel(
                             nc.scalar.activation(
                                 out=squares[:, head], in_=y[:, head], func=ACT.Square, accum_out=sumsq[:, h : h + 1]
                             )
-                        rms = work.tile([P, HEADS], F32, name="rms")
-                        nc.scalar.activation(out=rms[:], in_=sumsq[:], func=ACT.Sqrt, scale=1.0 / DH, bias=eps[:])
                         rinv = work.tile([P, HEADS], F32, name="rinv")
-                        nc.vector.reciprocal(out=rinv[:], in_=rms[:])
+                        nc.scalar.activation(
+                            out=rinv[:], in_=sumsq[:], func=ACT.Abs_reciprocal_sqrt, scale=1.0 / DH, bias=eps[:]
+                        )
 
                         for h in range(HEADS):
-                            head = slice((qk * HEADS + h) * DH, (qk * HEADS + h + 1) * DH)
-                            y_pairs = y[:, h * DH : (h + 1) * DH].rearrange("p (j c) -> p j c", c=2)
-                            for c in range(2):
-                                nc.vector.scalar_tensor_tensor(
-                                    out=part[:, c, head].rearrange("p (j i) -> p j i", i=2),
-                                    in0=y_pairs[:, :, c : c + 1].to_broadcast([P, PAIRS, 2]),
-                                    scalar=rinv[:, h : h + 1],
-                                    in1=coef[:, g, r, qk, c * DH : (c + 1) * DH].rearrange("p (j i) -> p j i", i=2),
-                                    op0=ALU.mult,
-                                    op1=ALU.mult,
-                                )
+                            nc.vector.scalar_tensor_tensor(
+                                out=part[:, qk * HEADS + h, :].rearrange("p (n i) -> p n i", i=2),
+                                in0=y[:, h * DH : (h + 1) * DH].unsqueeze(2).to_broadcast([P, DH, 2]),
+                                scalar=rinv[:, h : h + 1],
+                                in1=coef[:, g, r, qk, :].rearrange("p (n i) -> p n i", i=2),
+                                op0=ALU.mult,
+                                op1=ALU.mult,
+                            )
 
+                    pairs = part[:].rearrange("p m (j c i) -> p m j c i", c=2, i=2)
                     nc.gpsimd.tensor_tensor(
-                        out=result[:, 0:2, :, r, :].rearrange("p w h d -> p (w h) d"),
-                        in0=part[:, 0, :].rearrange("p (m d) -> p m d", d=DH),
-                        in1=part[:, 1, :].rearrange("p (m d) -> p m d", d=DH),
+                        out=result[:, 0:2, :, r, :].rearrange("p w h (j i) -> p (w h) j i", i=2),
+                        in0=pairs[:, :, :, 0, :],
+                        in1=pairs[:, :, :, 1, :],
                         op=ALU.add,
                     )
 

@@ -25,6 +25,7 @@ ROWS = 2
 UNIT = P * ROWS
 GROUPS = 1024 // UNIT
 EPS = 1e-6
+VALUE_PASSES = 3
 
 FLOPS = 2 * BATCH * 1024 * K * 3 * BLOCK
 
@@ -207,15 +208,16 @@ def tile_fluxjointattention_pa_t_kernel(
                     tokens = slice(r * P, (r + 1) * P)
 
                     v_bank = v_psum.tile([P, BLOCK], F32, name="v_bank")
-                    nc.tensor.matmul_mx(
-                        out=v_bank[:],
-                        lhsT=x_codes[:, tokens].bitcast(FP8X4),
-                        lhsT_scale=x_scales[:, tokens],
-                        rhs=w_codes[:, s, 2 * BLOCK :].bitcast(FP8X4),
-                        rhs_scale=w_scales[:, s, 2 * BLOCK :],
-                        start=True,
-                        stop=True,
-                    )
+                    for again in range(VALUE_PASSES):
+                        nc.tensor.matmul_mx(
+                            out=v_bank[:],
+                            lhsT=x_codes[:, tokens].bitcast(FP8X4),
+                            lhsT_scale=x_scales[:, tokens],
+                            rhs=w_codes[:, s, 2 * BLOCK :].bitcast(FP8X4),
+                            rhs_scale=w_scales[:, s, 2 * BLOCK :],
+                            start=True,
+                            stop=True,
+                        )
                     nc.vector.tensor_tensor(
                         out=result[:, 2, :, r, :],
                         in0=v_bank[:].rearrange("p (h d) -> p h d", h=HEADS),

@@ -24,8 +24,10 @@ VECTORS = 3 * HEADS
 ROWS = 2
 UNIT = P * ROWS
 GROUPS = 1024 // UNIT
+UNITS = GROUPS * BATCH
+SLOTS = 4 * UNITS
 EPS = 1e-6
-VALUE_PASSES = 3
+VALUE_PASSES = 1
 
 FLOPS = 2 * BATCH * 1024 * K * 3 * BLOCK
 
@@ -57,29 +59,53 @@ def tile_fluxjointattention_pa_t_kernel(
     with ExitStack() as stack:
         keep = stack.enter_context(tc.tile_pool(name="keep", bufs=1))
         stage = stack.enter_context(tc.tile_pool(name="stage", bufs=2))
+        codes_pool = stack.enter_context(tc.tile_pool(name="codes_pool", bufs=3))
         work = stack.enter_context(tc.tile_pool(name="work", bufs=3))
+        small = stack.enter_context(tc.tile_pool(name="small", bufs=4))
         turn_psum = stack.enter_context(tc.psum_pool(name="turn_psum", bufs=2))
         qk_psum = stack.enter_context(tc.psum_pool(name="qk_psum", bufs=2))
         back_psum = stack.enter_context(tc.psum_pool(name="back_psum", bufs=3))
         v_psum = stack.enter_context(tc.psum_pool(name="v_psum", bufs=1))
+        stack.enter_context(tc.manual_schedule())
+
+        def place(u):
+            g, b = divmod(u, BATCH)
+            return g, b, (0 if g == 0 else 1)
 
         ident = keep.tile([P, P], F32)
         make_identity(nc, ident[:])
         eps = keep.tile([P, 1], F32)
         nc.vector.memset(eps[:], EPS)
+        bias_rows = keep.tile([P, P], BF16)
+        nc.vector.memset(bias_rows[:], 0.0)
+
+        gain_raw = {}
+        v_bias_raw = {}
+        for s in range(2):
+            nc.scalar.dma_start(
+                out=bias_rows[s * VECTORS : (s + 1) * VECTORS, :], in_=biases[s].rearrange("(m n) -> m n", n=DH)
+            )
+        for s in range(2):
+            for qk in range(2):
+                gain_raw[s, qk] = keep.tile([P, DH], BF16, name="gain_raw_%d_%d" % (s, qk))
+            v_bias_raw[s] = keep.tile([P, BLOCK], BF16, name="v_bias_raw_%d" % s)
+        for qk in range(2):
+            nc.scalar.dma_start(out=gain_raw[0, qk][:], in_=gains[0][qk].partition_broadcast(P))
         warm = keep.tile([P, 1], F32)
         nc.scalar.activation(out=warm[:], in_=eps[:], func=ACT.Abs_reciprocal_sqrt)
 
         x_raw = {}
         w_raw = {}
+        rope_raw = {}
 
-        def load_tokens(g, b):
-            s, first = (0, 0) if g == 0 else (1, (g - 1) * UNIT)
-            rows = keep.tile([P, ROWS, K], BF16, name="x_raw_%d_%d" % (g, b))
+        def load_tokens(u):
+            g, b, s = place(u)
+            first = 0 if g == 0 else (g - 1) * UNIT
+            rows = keep.tile([P, ROWS, K], BF16, name="x_raw_%d" % u)
             nc.sync.dma_start(
                 out=rows[:], in_=hidden[s][b, first : first + UNIT, :].rearrange("(p r) k -> p r k", r=ROWS)
             )
-            x_raw[g, b] = rows
+            x_raw[u] = rows
 
         def load_weight_block(s, blk):
             rows = keep.tile([P, HEADS, K], BF16, name="w_raw_%d_%d" % (s, blk))
@@ -88,183 +114,308 @@ def tile_fluxjointattention_pa_t_kernel(
             )
             w_raw[s, blk] = rows
 
-        load_tokens(0, 0)
+        def load_rope(g):
+            rows = keep.tile([P, ROWS, PACK * PAIRS], BF16, name="rope_raw_%d" % g)
+            nc.sync.dma_start(
+                out=rows[:],
+                in_=image_rotary_emb[0, 0, g * UNIT : (g + 1) * UNIT].rearrange("(p r) j i c -> p r (j i c)", r=ROWS),
+            )
+            rope_raw[g] = rows
+
+        load_tokens(0)
+        load_rope(0)
         for blk in range(3):
             load_weight_block(0, blk)
-        rope_raw = keep.tile([P, GROUPS, ROWS, PACK * PAIRS], BF16)
-        nc.sync.dma_start(
-            out=rope_raw[:],
-            in_=image_rotary_emb.rearrange("x y (g p r) j i c -> p (x y g) r (j i c)", g=GROUPS, r=ROWS),
-        )
-        for b in range(1, BATCH):
-            load_tokens(0, b)
+        nc.sync.dma_start(out=v_bias_raw[0][:], in_=biases[0][2 * BLOCK :].partition_broadcast(P))
+        load_tokens(1)
+        load_tokens(2)
+        load_tokens(3)
+        for qk in range(2):
+            nc.sync.dma_start(out=gain_raw[1, qk][:], in_=gains[1][qk].partition_broadcast(P))
+        load_rope(1)
         for blk in range(3):
             load_weight_block(1, blk)
-        for g in range(1, GROUPS):
-            for b in range(BATCH):
-                load_tokens(g, b)
-
-        bias_rows = keep.tile([P, P], BF16)
-        nc.vector.memset(bias_rows[:], 0.0)
-        v_bias_raw = keep.tile([P, 2, BLOCK], BF16)
-        gain_raw = keep.tile([P, 2, 2, DH], BF16)
-        for s in range(2):
-            nc.scalar.dma_start(
-                out=bias_rows[s * VECTORS : (s + 1) * VECTORS, :], in_=biases[s].rearrange("(m n) -> m n", n=DH)
-            )
-            nc.scalar.dma_start(out=v_bias_raw[:, s, :], in_=biases[s][2 * BLOCK :].partition_broadcast(P))
-            for qk in range(2):
-                nc.scalar.dma_start(out=gain_raw[:, s, qk, :], in_=gains[s][qk].partition_broadcast(P))
-
-        v_bias = keep.tile([P, 2, BLOCK], F32)
-        coef = keep.tile([P, GROUPS, ROWS, 2, 2 * DH], F32)
-        w_codes = keep.tile([P, 2, 3 * BLOCK], U32, align_bytes=64)
-        w_scales = keep.tile([P, 2, 3 * BLOCK], U8, align_bytes=64)
-
-        def prepare_tables(s, eng):
-            eng.tensor_copy(out=v_bias[:, s, :], in_=v_bias_raw[:, s, :])
-            for g in range(GROUPS):
-                if (g == 0) != (s == 0):
-                    continue
-                for r in range(ROWS):
-                    for qk in range(2):
-                        eng.tensor_tensor(
-                            out=coef[:, g, r, qk, :].rearrange("p (j c i) -> p j c i", c=2, i=2),
-                            in0=rope_raw[:, g, r, :].rearrange("p (j i c) -> p j c i", i=2, c=2),
-                            in1=gain_raw[:, s, qk, :]
-                            .rearrange("p (j c) -> p j c", c=2)
-                            .unsqueeze(3)
-                            .to_broadcast([P, PAIRS, 2, 2]),
-                            op=ALU.mult,
-                        )
-
-        def turn_and_group(raw_rows, words):
-            turned = turn_psum.tile([P, 2, HALVES, P], F32, name="turned")
-            for t in range(2):
-                for u in range(HALVES):
-                    nc.tensor.transpose(turned[:, t, u, :], raw_rows(t)[:, u * P : (u + 1) * P], ident[:])
-            nc.scalar.copy(out=words, in_=turned[:].rearrange("p t u n -> p t n u"))
-
-        def quantise_weight_block(s, blk):
-            grouped = stage.tile([P, BLOCK * PACK], BF16, align_bytes=64, name="w_grouped")
-            words = grouped[:].bitcast(F32).rearrange("p (h n u) -> p h n u", h=HEADS, u=HALVES)
-            for first in range(0, HEADS, 2):
-                turn_and_group(lambda t: w_raw[s, blk][:, first + t, :].bitcast(F32), words[:, first : first + 2])
-            cols = slice(blk * BLOCK, (blk + 1) * BLOCK)
-            nc.vector.quantize_mx(
-                out=w_codes[:, s, cols].bitcast(FP8X4), scales=w_scales[:, s, cols], in_=grouped[:]
-            )
-
-        def quantise_tokens(g, b):
-            grouped = stage.tile([P, UNIT * PACK], BF16, align_bytes=64, name="x_grouped")
-            words = grouped[:].bitcast(F32).rearrange("p (r n u) -> p r n u", r=ROWS, u=HALVES)
-            turn_and_group(lambda r: x_raw[g, b][:, r, :].bitcast(F32), words)
-            codes = work.tile([P, UNIT], U32, align_bytes=64, name="x_codes")
-            scales = work.tile([P, UNIT], U8, align_bytes=64, name="x_scales")
-            nc.vector.quantize_mx(out=codes[:].bitcast(FP8X4), scales=scales[:], in_=grouped[:])
-            return codes, scales
+        nc.sync.dma_start(out=v_bias_raw[1][:], in_=biases[1][2 * BLOCK :].partition_broadcast(P))
+        load_tokens(4)
+        load_tokens(5)
+        load_rope(2)
+        load_rope(3)
+        for u in range(6, UNITS):
+            load_tokens(u)
 
         bias_cols = keep.tile([P, P], F32)
-        for g in range(GROUPS):
+        bias_rows_f32 = keep.tile([P, P], F32)
+        nc.vector.tensor_copy(out=bias_rows_f32[:], in_=bias_rows[:])
+        bias_turned = turn_psum.tile([P, P], F32, name="turned")
+        nc.tensor.transpose(bias_turned[:], bias_rows_f32[:], ident[:])
+        nc.vector.tensor_copy(out=bias_cols[:], in_=bias_turned[:])
+
+        v_bias = {}
+        coef = {}
+
+        def table_v_bias(s):
+            v_bias[s] = keep.tile([P, BLOCK], F32, name="v_bias_%d" % s)
+            nc.gpsimd.tensor_copy(out=v_bias[s][:], in_=v_bias_raw[s][:])
+
+        def table_coef(g, r, qk):
             s = 0 if g == 0 else 1
-            if g < 2:
-                prepare_tables(s, nc.vector if s == 0 else nc.gpsimd)
-                for blk in range(3):
-                    quantise_weight_block(s, blk)
-            if g == 0:
-                bias_rows_f32 = keep.tile([P, P], F32)
-                nc.vector.tensor_copy(out=bias_rows_f32[:], in_=bias_rows[:])
-                bias_turned = turn_psum.tile([P, P], F32, name="turned")
-                nc.tensor.transpose(bias_turned[:], bias_rows_f32[:], ident[:])
-                nc.vector.tensor_copy(out=bias_cols[:], in_=bias_turned[:])
-            for b in range(BATCH):
-                x_codes, x_scales = quantise_tokens(g, b)
-                result = work.tile([P, 3, HEADS, ROWS, DH], F32, name="result")
+            coef[g, r, qk] = keep.tile([P, 2 * DH], F32, name="coef_%d_%d_%d" % (g, r, qk))
+            nc.gpsimd.tensor_tensor(
+                out=coef[g, r, qk][:].rearrange("p (j c i) -> p j c i", c=2, i=2),
+                in0=rope_raw[g][:, r, :].rearrange("p (j i c) -> p j c i", i=2, c=2),
+                in1=gain_raw[s, qk][:].rearrange("p (j c) -> p j c", c=2).unsqueeze(3).to_broadcast([P, PAIRS, 2, 2]),
+                op=ALU.mult,
+            )
 
-                y_turned = work.tile([P, 2 * HEADS, UNIT], F32, name="y_turned")
-                for first in range(0, 2 * HEADS, 2):
-                    qk_bank = qk_psum.tile([P, 2, UNIT], F32, name="qk_bank")
-                    for t in range(2):
-                        m = first + t
-                        nc.tensor.matmul_mx(
-                            out=qk_bank[:, t, :],
-                            lhsT=w_codes[:, s, m * DH : (m + 1) * DH].bitcast(FP8X4),
-                            lhsT_scale=w_scales[:, s, m * DH : (m + 1) * DH],
-                            rhs=x_codes[:].bitcast(FP8X4),
-                            rhs_scale=x_scales[:],
-                            start=True,
-                            stop=True,
-                        )
-                    for t in range(2):
-                        m = first + t
-                        nc.scalar.activation(
-                            out=y_turned[:, m, :],
-                            in_=qk_bank[:, t, :],
-                            func=ACT.Identity,
-                            bias=bias_cols[:, s * VECTORS + m : s * VECTORS + m + 1],
-                        )
+        turned_x = {}
+        grouped_x = {}
+        x_codes = {}
+        x_scales = {}
+        turned_w = {}
+        grouped_w = {}
+        w_codes = {}
+        w_scales = {}
+        qk_bank = {}
+        y_turned = {}
+        y_bank = {}
+        sumsq = {}
+        rinv = {}
+        part = {}
+        res = {}
+        v_bank = {}
 
-                for r in range(ROWS):
-                    tokens = slice(r * P, (r + 1) * P)
+        def turn(pool, tag, raw_rows):
+            turned = pool.tile([P, 2, HALVES, P], F32, name=tag)
+            for t in range(2):
+                for v in range(HALVES):
+                    nc.tensor.transpose(turned[:, t, v, :], raw_rows(t)[:, v * P : (v + 1) * P], ident[:])
+            return turned
 
-                    v_bank = v_psum.tile([P, BLOCK], F32, name="v_bank")
-                    for again in range(VALUE_PASSES):
-                        nc.tensor.matmul_mx(
-                            out=v_bank[:],
-                            lhsT=x_codes[:, tokens].bitcast(FP8X4),
-                            lhsT_scale=x_scales[:, tokens],
-                            rhs=w_codes[:, s, 2 * BLOCK :].bitcast(FP8X4),
-                            rhs_scale=w_scales[:, s, 2 * BLOCK :],
-                            start=True,
-                            stop=True,
-                        )
-                    nc.vector.tensor_tensor(
-                        out=result[:, 2, :, r, :],
-                        in0=v_bank[:].rearrange("p (h d) -> p h d", h=HEADS),
-                        in1=v_bias[:, s, :].rearrange("p (h d) -> p h d", h=HEADS),
-                        op=ALU.add,
-                    )
+        def group(on_vector, turned, words):
+            src = turned[:].rearrange("p t u n -> p t n u")
+            if on_vector:
+                nc.vector.tensor_copy(out=words, in_=src)
+            else:
+                nc.scalar.copy(out=words, in_=src)
 
-                    part = work.tile([P, 2 * HEADS, 2 * DH], F32, name="part")
-                    for qk in range(2):
-                        y = back_psum.tile([P, BLOCK], F32, name="y")
-                        for h in range(HEADS):
-                            nc.tensor.transpose(
-                                y[:, h * DH : (h + 1) * DH], y_turned[:, qk * HEADS + h, tokens], ident[:]
-                            )
+        def t_in(u):
+            turned_x[u] = turn(turn_psum, "turned", lambda r: x_raw[u][:, r, :].bitcast(F32))
 
-                        squares = work.tile([P, BLOCK], BF16, name="squares")
-                        sumsq = work.tile([P, HEADS], F32, name="sumsq")
-                        for h in range(HEADS):
-                            head = slice(h * DH, (h + 1) * DH)
-                            nc.scalar.activation(
-                                out=squares[:, head], in_=y[:, head], func=ACT.Square, accum_out=sumsq[:, h : h + 1]
-                            )
-                        rinv = work.tile([P, HEADS], F32, name="rinv")
-                        nc.scalar.activation(
-                            out=rinv[:], in_=sumsq[:], func=ACT.Abs_reciprocal_sqrt, scale=1.0 / DH, bias=eps[:]
-                        )
+        def s_in(u):
+            grouped_x[u] = stage.tile([P, UNIT * PACK], BF16, align_bytes=64, name="x_grouped")
+            group(False, turned_x[u], grouped_x[u][:].bitcast(F32).rearrange("p (r n u) -> p r n u", r=ROWS, u=HALVES))
 
-                        for h in range(HEADS):
-                            nc.vector.scalar_tensor_tensor(
-                                out=part[:, qk * HEADS + h, :].rearrange("p (n i) -> p n i", i=2),
-                                in0=y[:, h * DH : (h + 1) * DH].unsqueeze(2).to_broadcast([P, DH, 2]),
-                                scalar=rinv[:, h : h + 1],
-                                in1=coef[:, g, r, qk, :].rearrange("p (n i) -> p n i", i=2),
-                                op0=ALU.mult,
-                                op1=ALU.mult,
-                            )
+        def v_quant(u):
+            x_codes[u] = codes_pool.tile([P, UNIT], U32, align_bytes=64, name="x_codes")
+            x_scales[u] = codes_pool.tile([P, UNIT], U8, align_bytes=64, name="x_scales")
+            nc.vector.quantize_mx(out=x_codes[u][:].bitcast(FP8X4), scales=x_scales[u][:], in_=grouped_x[u][:])
 
-                    pairs = part[:].rearrange("p m (j c i) -> p m j c i", c=2, i=2)
-                    nc.gpsimd.tensor_tensor(
-                        out=result[:, 0:2, :, r, :].rearrange("p w h (j i) -> p (w h) j i", i=2),
-                        in0=pairs[:, :, :, 0, :],
-                        in1=pairs[:, :, :, 1, :],
-                        op=ALU.add,
-                    )
+        def t_w(s, k, pool, tag):
+            turned_w[s, k] = turn(pool, tag, lambda t: w_raw[s, k // 2][:, 2 * (k % 2) + t, :].bitcast(F32))
 
-                for which in range(3):
-                    nc.sync.dma_start(
-                        out=outs[which][b, :, g * UNIT : (g + 1) * UNIT, :].rearrange("h (p r) d -> p h (r d)", r=ROWS),
-                        in_=result[:, which].rearrange("p h r d -> p h (r d)"),
-                    )
+        def c_w(s, k, on_vector):
+            piece = min(k, 4)
+            if k <= 4:
+                width = 2 * DH if k < 4 else BLOCK
+                grouped_w[s, piece] = stage.tile([P, width * PACK], BF16, align_bytes=64, name="w_grouped")
+            words = grouped_w[s, piece][:].bitcast(F32).rearrange("p (h n u) -> p h n u", n=DH, u=HALVES)
+            first = 2 * (k - piece)
+            group(on_vector, turned_w[s, k], words[:, first : first + 2])
+
+        def q_w(s, piece):
+            width = 2 * DH if piece < 4 else BLOCK
+            w_codes[s, piece] = keep.tile([P, width], U32, align_bytes=64, name="w_codes_%d_%d" % (s, piece))
+            w_scales[s, piece] = keep.tile([P, width], U8, align_bytes=64, name="w_scales_%d_%d" % (s, piece))
+            nc.vector.quantize_mx(
+                out=w_codes[s, piece][:].bitcast(FP8X4), scales=w_scales[s, piece][:], in_=grouped_w[s, piece][:]
+            )
+
+        def t_qk(u, j):
+            s = place(u)[2]
+            qk_bank[u, j] = qk_psum.tile([P, 2, UNIT], F32, name="qk_bank")
+            for t in range(2):
+                nc.tensor.matmul_mx(
+                    out=qk_bank[u, j][:, t, :],
+                    lhsT=w_codes[s, j][:, t * DH : (t + 1) * DH].bitcast(FP8X4),
+                    lhsT_scale=w_scales[s, j][:, t * DH : (t + 1) * DH],
+                    rhs=x_codes[u][:].bitcast(FP8X4),
+                    rhs_scale=x_scales[u][:],
+                    start=True,
+                    stop=True,
+                )
+
+        def s_evac(u, j, t):
+            s = place(u)[2]
+            if j == 0 and t == 0:
+                y_turned[u] = stage.tile([P, 2 * HEADS, UNIT], F32, name="y_turned")
+            m = 2 * j + t
+            nc.scalar.activation(
+                out=y_turned[u][:, m, :],
+                in_=qk_bank[u, j][:, t, :],
+                func=ACT.Identity,
+                bias=bias_cols[:, s * VECTORS + m : s * VECTORS + m + 1],
+            )
+
+        def where(slot):
+            u, i = divmod(slot, 4)
+            qk, r = divmod(i, 2)
+            return u, qk, r
+
+        def t_back(slot):
+            u, qk, r = where(slot)
+            y_bank[slot] = back_psum.tile([P, BLOCK], F32, name="y")
+            for h in range(HEADS):
+                nc.tensor.transpose(
+                    y_bank[slot][:, h * DH : (h + 1) * DH], y_turned[u][:, qk * HEADS + h, r * P : (r + 1) * P], ident[:]
+                )
+
+        def s_squares(slot):
+            squares = work.tile([P, BLOCK], BF16, name="squares")
+            sumsq[slot] = small.tile([P, HEADS], F32, name="sumsq")
+            for h in range(HEADS):
+                head = slice(h * DH, (h + 1) * DH)
+                nc.scalar.activation(
+                    out=squares[:, head], in_=y_bank[slot][:, head], func=ACT.Square, accum_out=sumsq[slot][:, h : h + 1]
+                )
+
+        def s_rinv(slot):
+            rinv[slot] = small.tile([P, HEADS], F32, name="rinv")
+            nc.scalar.activation(
+                out=rinv[slot][:], in_=sumsq[slot][:], func=ACT.Abs_reciprocal_sqrt, scale=1.0 / DH, bias=eps[:]
+            )
+
+        def v_part(slot):
+            u, qk, r = where(slot)
+            g = place(u)[0]
+            part[slot] = work.tile([P, HEADS, 2 * DH], F32, name="part")
+            for h in range(HEADS):
+                nc.vector.scalar_tensor_tensor(
+                    out=part[slot][:, h, :].rearrange("p (n i) -> p n i", i=2),
+                    in0=y_bank[slot][:, h * DH : (h + 1) * DH].unsqueeze(2).to_broadcast([P, DH, 2]),
+                    scalar=rinv[slot][:, h : h + 1],
+                    in1=coef[g, r, qk][:].rearrange("p (n i) -> p n i", i=2),
+                    op0=ALU.mult,
+                    op1=ALU.mult,
+                )
+
+        def g_add(slot):
+            u, qk, r = where(slot)
+            if r == 0:
+                res[u, qk] = work.tile([P, HEADS, ROWS, DH], F32, name="res_%d" % qk)
+            pairs = part[slot][:].rearrange("p h (j c i) -> p h j c i", c=2, i=2)
+            nc.gpsimd.tensor_tensor(
+                out=res[u, qk][:, :, r, :].rearrange("p h (j i) -> p h j i", i=2),
+                in0=pairs[:, :, :, 0, :],
+                in1=pairs[:, :, :, 1, :],
+                op=ALU.add,
+            )
+
+        def t_v(u, r):
+            s = place(u)[2]
+            v_bank[u, r] = v_psum.tile([P, BLOCK], F32, name="v_bank")
+            for again in range(VALUE_PASSES):
+                nc.tensor.matmul_mx(
+                    out=v_bank[u, r][:],
+                    lhsT=x_codes[u][:, r * P : (r + 1) * P].bitcast(FP8X4),
+                    lhsT_scale=x_scales[u][:, r * P : (r + 1) * P],
+                    rhs=w_codes[s, 4][:].bitcast(FP8X4),
+                    rhs_scale=w_scales[s, 4][:],
+                    start=True,
+                    stop=True,
+                )
+
+        def v_values(u, r):
+            s = place(u)[2]
+            if r == 0:
+                res[u, 2] = work.tile([P, HEADS, ROWS, DH], F32, name="res_2")
+            nc.vector.tensor_tensor(
+                out=res[u, 2][:, :, r, :],
+                in0=v_bank[u, r][:].rearrange("p (h d) -> p h d", h=HEADS),
+                in1=v_bias[s][:].rearrange("p (h d) -> p h d", h=HEADS),
+                op=ALU.add,
+            )
+
+        def store(u, which):
+            g, b, s = place(u)
+            nc.sync.dma_start(
+                out=outs[which][b, :, g * UNIT : (g + 1) * UNIT, :].rearrange("h (p r) d -> p h (r d)", r=ROWS),
+                in_=res[u, which][:].rearrange("p h r d -> p h (r d)"),
+            )
+
+        w_turn = {}
+        w_copy = {}
+        w_quant = {}
+        for k in range(6):
+            w_turn.setdefault(k - 6, []).append((0, k, k < 4))
+            w_copy.setdefault(k - 6, []).append((0, k, k % 2 == 0))
+            if k != 4:
+                w_quant.setdefault(k - 6, []).append((0, min(k, 4)))
+            at = (5, 6, 7, 9, 10, 11)[k]
+            w_turn.setdefault(at, []).append((1, k, False))
+            w_copy.setdefault(at + 1, []).append((1, k, k % 2 == 1))
+            if k != 4:
+                w_quant.setdefault(at + 2, []).append((1, min(k, 4)))
+        tables = {}
+        later = [(1, r, qk) for qk in range(2) for r in range(ROWS)] + [None]
+        later += [(g, r, qk) for g in range(2, GROUPS) for qk in range(2) for r in range(ROWS)]
+        for n, what in enumerate(later):
+            tables[2 + 3 * n] = what
+
+        for qk in range(2):
+            for r in range(ROWS):
+                table_coef(0, r, qk)
+        table_v_bias(0)
+
+        for slot in range(-8, SLOTS + 2):
+            u, i = divmod(slot, 4)
+            live = 0 <= slot < SLOTS
+            ahead = 0 <= u + 1 < UNITS
+            far = 0 <= u + 2 < UNITS
+            if ahead:
+                t_qk(u + 1, i)
+            if 0 <= slot + 1 < SLOTS:
+                t_back(slot + 1)
+            if i == 0 and far:
+                t_in(u + 2)
+            for s, k, in_back in w_turn.get(slot, []):
+                if in_back:
+                    t_w(s, k, back_psum, "y")
+                else:
+                    t_w(s, k, turn_psum, "turned")
+            if live and i % 2 == 0:
+                t_v(u, i // 2)
+            if live:
+                s_squares(slot)
+            if ahead:
+                s_evac(u + 1, i, 0)
+            if live:
+                s_rinv(slot)
+            if ahead:
+                s_evac(u + 1, i, 1)
+            if i == 1 and far:
+                s_in(u + 2)
+            for s, k, on_vector in w_copy.get(slot, []):
+                if not on_vector:
+                    c_w(s, k, False)
+            if 0 <= slot - 1 < SLOTS:
+                v_part(slot - 1)
+            if live and i % 2 == 1:
+                v_values(u, i // 2)
+            if i == 2 and far:
+                v_quant(u + 2)
+            for s, k, on_vector in w_copy.get(slot, []):
+                if on_vector:
+                    c_w(s, k, True)
+            for s, piece in w_quant.get(slot, []):
+                q_w(s, piece)
+            if 0 <= slot - 1 < SLOTS:
+                g_add(slot - 1)
+            if slot in tables:
+                if tables[slot] is None:
+                    table_v_bias(1)
+                else:
+                    table_coef(tables[slot][0], tables[slot][1], tables[slot][2])
+            if 0 <= slot - 1 < SLOTS and (slot - 1) % 2 == 1:
+                store((slot - 1) // 4, ((slot - 1) % 4) // 2)
+            if live and i == 3:
+                store(u, 2)

@@ -28,6 +28,7 @@ UNITS = GROUPS * BATCH
 SLOTS = 4 * UNITS
 EPS = 1e-6
 VALUE_PASSES = 1
+QK_PASSES = 1
 
 FLOPS = 2 * BATCH * 1024 * K * 3 * BLOCK
 
@@ -74,6 +75,10 @@ def tile_fluxjointattention_pa_t_kernel(
 
         ident = keep.tile([P, P], F32)
         make_identity(nc, ident[:])
+        pairs_apart = keep.tile([P, P], F32)
+        nc.gpsimd.tensor_copy(
+            out=pairs_apart[:].rearrange("p (c j) -> p c j", c=2), in_=ident[:].rearrange("p (j c) -> p c j", c=2)
+        )
         eps = keep.tile([P, 1], F32)
         nc.vector.memset(eps[:], EPS)
         bias_rows = keep.tile([P, P], BF16)
@@ -161,9 +166,9 @@ def tile_fluxjointattention_pa_t_kernel(
             s = 0 if g == 0 else 1
             coef[g, r, qk] = keep.tile([P, 2 * DH], F32, name="coef_%d_%d_%d" % (g, r, qk))
             nc.gpsimd.tensor_tensor(
-                out=coef[g, r, qk][:].rearrange("p (j c i) -> p j c i", c=2, i=2),
-                in0=rope_raw[g][:, r, :].rearrange("p (j i c) -> p j c i", i=2, c=2),
-                in1=gain_raw[s, qk][:].rearrange("p (j c) -> p j c", c=2).unsqueeze(3).to_broadcast([P, PAIRS, 2, 2]),
+                out=coef[g, r, qk][:].rearrange("p (c j i) -> p c j i", c=2, i=2),
+                in0=rope_raw[g][:, r, :].rearrange("p (j i c) -> p c j i", i=2, c=2),
+                in1=gain_raw[s, qk][:].rearrange("p (j c) -> p c j", c=2).unsqueeze(3).to_broadcast([P, 2, PAIRS, 2]),
                 op=ALU.mult,
             )
 
@@ -201,7 +206,7 @@ def tile_fluxjointattention_pa_t_kernel(
         def t_in(u):
             turned_x[u] = turn(turn_psum, "turned", lambda r: x_raw[u][:, r, :].bitcast(F32))
 
-        def s_in(u):
+        def c_in(u):
             grouped_x[u] = stage.tile([P, UNIT * PACK], BF16, align_bytes=64, name="x_grouped")
             group(False, turned_x[u], grouped_x[u][:].bitcast(F32).rearrange("p (r n u) -> p r n u", r=ROWS, u=HALVES))
 
@@ -233,7 +238,7 @@ def tile_fluxjointattention_pa_t_kernel(
         def t_qk(u, j):
             s = place(u)[2]
             qk_bank[u, j] = qk_psum.tile([P, 2, UNIT], F32, name="qk_bank")
-            for t in range(2):
+            for t in [t for again in range(QK_PASSES) for t in range(2)]:
                 nc.tensor.matmul_mx(
                     out=qk_bank[u, j][:, t, :],
                     lhsT=w_codes[s, j][:, t * DH : (t + 1) * DH].bitcast(FP8X4),
@@ -266,7 +271,7 @@ def tile_fluxjointattention_pa_t_kernel(
             y_bank[slot] = back_psum.tile([P, BLOCK], F32, name="y")
             for h in range(HEADS):
                 nc.tensor.transpose(
-                    y_bank[slot][:, h * DH : (h + 1) * DH], y_turned[u][:, qk * HEADS + h, r * P : (r + 1) * P], ident[:]
+                    y_bank[slot][:, h * DH : (h + 1) * DH], y_turned[u][:, qk * HEADS + h, r * P : (r + 1) * P], pairs_apart[:]
                 )
 
         def s_squares(slot):
@@ -287,10 +292,11 @@ def tile_fluxjointattention_pa_t_kernel(
         def v_part(slot):
             u, qk, r = where(slot)
             g = place(u)[0]
-            part[slot] = work.tile([P, HEADS, 2 * DH], F32, name="part")
+            if r == 0:
+                part[u, qk] = work.tile([P, HEADS, ROWS, 2 * DH], F32, name="part")
             for h in range(HEADS):
                 nc.vector.scalar_tensor_tensor(
-                    out=part[slot][:, h, :].rearrange("p (n i) -> p n i", i=2),
+                    out=part[u, qk][:, h, r, :].rearrange("p (n i) -> p n i", i=2),
                     in0=y_bank[slot][:, h * DH : (h + 1) * DH].unsqueeze(2).to_broadcast([P, DH, 2]),
                     scalar=rinv[slot][:, h : h + 1],
                     in1=coef[g, r, qk][:].rearrange("p (n i) -> p n i", i=2),
@@ -298,15 +304,13 @@ def tile_fluxjointattention_pa_t_kernel(
                     op1=ALU.mult,
                 )
 
-        def g_add(slot):
-            u, qk, r = where(slot)
-            if r == 0:
-                res[u, qk] = work.tile([P, HEADS, ROWS, DH], F32, name="res_%d" % qk)
-            pairs = part[slot][:].rearrange("p h (j c i) -> p h j c i", c=2, i=2)
+        def g_add(u, qk):
+            res[u, qk] = work.tile([P, HEADS, ROWS, DH], F32, name="res_%d" % qk)
+            planes = part[u, qk][:].rearrange("p h r (c n) -> p (h r) c n", c=2)
             nc.gpsimd.tensor_tensor(
-                out=res[u, qk][:, :, r, :].rearrange("p h (j i) -> p h j i", i=2),
-                in0=pairs[:, :, :, 0, :],
-                in1=pairs[:, :, :, 1, :],
+                out=res[u, qk][:].rearrange("p h r n -> p (h r) n"),
+                in0=planes[:, :, 0, :],
+                in1=planes[:, :, 1, :],
                 op=ALU.add,
             )
 
@@ -393,7 +397,7 @@ def tile_fluxjointattention_pa_t_kernel(
             if ahead:
                 s_evac(u + 1, i, 1)
             if i == 1 and far:
-                s_in(u + 2)
+                c_in(u + 2)
             for s, k, on_vector in w_copy.get(slot, []):
                 if not on_vector:
                     c_w(s, k, False)
@@ -408,8 +412,8 @@ def tile_fluxjointattention_pa_t_kernel(
                     c_w(s, k, True)
             for s, piece in w_quant.get(slot, []):
                 q_w(s, piece)
-            if 0 <= slot - 1 < SLOTS:
-                g_add(slot - 1)
+            if 0 <= slot - 1 < SLOTS and (slot - 1) % 2 == 1:
+                g_add((slot - 1) // 4, ((slot - 1) % 4) // 2)
             if slot in tables:
                 if tables[slot] is None:
                     table_v_bias(1)

@@ -60,13 +60,13 @@ def tile_fluxjointattention_pa_t_kernel(
     with ExitStack() as stack:
         keep = stack.enter_context(tc.tile_pool(name="keep", bufs=1))
         stage = stack.enter_context(tc.tile_pool(name="stage", bufs=2))
-        codes_pool = stack.enter_context(tc.tile_pool(name="codes_pool", bufs=3))
+        codes_pool = stack.enter_context(tc.tile_pool(name="codes_pool", bufs=4))
         work = stack.enter_context(tc.tile_pool(name="work", bufs=3))
+        parts_pool = stack.enter_context(tc.tile_pool(name="parts_pool", bufs=4))
         small = stack.enter_context(tc.tile_pool(name="small", bufs=4))
-        turn_psum = stack.enter_context(tc.psum_pool(name="turn_psum", bufs=2))
+        turn_psum = stack.enter_context(tc.psum_pool(name="turn_psum", bufs=3))
         qk_psum = stack.enter_context(tc.psum_pool(name="qk_psum", bufs=2))
         back_psum = stack.enter_context(tc.psum_pool(name="back_psum", bufs=3))
-        v_psum = stack.enter_context(tc.psum_pool(name="v_psum", bufs=1))
         stack.enter_context(tc.manual_schedule())
 
         def place(u):
@@ -112,12 +112,12 @@ def tile_fluxjointattention_pa_t_kernel(
             )
             x_raw[u] = rows
 
-        def load_weight_block(s, blk):
-            rows = keep.tile([P, HEADS, K], BF16, name="w_raw_%d_%d" % (s, blk))
+        def load_weights(s, k):
+            rows = keep.tile([P, 2, K], BF16, name="w_raw_%d_%d" % (s, k))
             nc.sync.dma_start(
-                out=rows[:], in_=weights[s][blk * BLOCK : (blk + 1) * BLOCK, :].rearrange("(h p) k -> p h k", p=P)
+                out=rows[:], in_=weights[s][2 * k * DH : 2 * (k + 1) * DH, :].rearrange("(h p) k -> p h k", p=P)
             )
-            w_raw[s, blk] = rows
+            w_raw[s, k] = rows
 
         def load_rope(g):
             rows = keep.tile([P, ROWS, PACK * PAIRS], BF16, name="rope_raw_%d" % g)
@@ -128,18 +128,22 @@ def tile_fluxjointattention_pa_t_kernel(
             rope_raw[g] = rows
 
         load_tokens(0)
+        load_weights(0, 0)
+        load_weights(0, 1)
         load_rope(0)
-        for blk in range(3):
-            load_weight_block(0, blk)
-        nc.sync.dma_start(out=v_bias_raw[0][:], in_=biases[0][2 * BLOCK :].partition_broadcast(P))
+        load_weights(0, 2)
+        load_weights(0, 3)
         load_tokens(1)
+        load_weights(0, 4)
+        load_weights(0, 5)
+        nc.sync.dma_start(out=v_bias_raw[0][:], in_=biases[0][2 * BLOCK :].partition_broadcast(P))
         load_tokens(2)
-        load_tokens(3)
         for qk in range(2):
             nc.sync.dma_start(out=gain_raw[1, qk][:], in_=gains[1][qk].partition_broadcast(P))
         load_rope(1)
-        for blk in range(3):
-            load_weight_block(1, blk)
+        load_tokens(3)
+        for k in range(6):
+            load_weights(1, k)
         nc.sync.dma_start(out=v_bias_raw[1][:], in_=biases[1][2 * BLOCK :].partition_broadcast(P))
         load_tokens(4)
         load_tokens(5)
@@ -216,7 +220,7 @@ def tile_fluxjointattention_pa_t_kernel(
             nc.vector.quantize_mx(out=x_codes[u][:].bitcast(FP8X4), scales=x_scales[u][:], in_=grouped_x[u][:])
 
         def t_w(s, k, pool, tag):
-            turned_w[s, k] = turn(pool, tag, lambda t: w_raw[s, k // 2][:, 2 * (k % 2) + t, :].bitcast(F32))
+            turned_w[s, k] = turn(pool, tag, lambda t: w_raw[s, k][:, t, :].bitcast(F32))
 
         def c_w(s, k, on_vector):
             piece = min(k, 4)
@@ -249,17 +253,18 @@ def tile_fluxjointattention_pa_t_kernel(
                     stop=True,
                 )
 
-        def s_evac(u, j, t):
+        def evac(u, j, t, on_vector):
             s = place(u)[2]
             if j == 0 and t == 0:
                 y_turned[u] = stage.tile([P, 2 * HEADS, UNIT], F32, name="y_turned")
             m = 2 * j + t
-            nc.scalar.activation(
-                out=y_turned[u][:, m, :],
-                in_=qk_bank[u, j][:, t, :],
-                func=ACT.Identity,
-                bias=bias_cols[:, s * VECTORS + m : s * VECTORS + m + 1],
-            )
+            bias = bias_cols[:, s * VECTORS + m : s * VECTORS + m + 1]
+            if on_vector:
+                nc.vector.tensor_scalar(
+                    out=y_turned[u][:, m, :], in0=qk_bank[u, j][:, t, :], scalar1=bias, scalar2=None, op0=ALU.add
+                )
+            else:
+                nc.scalar.activation(out=y_turned[u][:, m, :], in_=qk_bank[u, j][:, t, :], func=ACT.Identity, bias=bias)
 
         def where(slot):
             u, i = divmod(slot, 4)
@@ -292,11 +297,16 @@ def tile_fluxjointattention_pa_t_kernel(
         def v_part(slot):
             u, qk, r = where(slot)
             g = place(u)[0]
-            if r == 0:
-                part[u, qk] = work.tile([P, HEADS, ROWS, 2 * DH], F32, name="part")
+            if slot >= SLOTS - 4:
+                part[slot] = parts_pool.tile([P, HEADS, 1, 2 * DH], F32, name="part")
+                mine = part[slot][:, :, 0, :]
+            else:
+                if r == 0:
+                    part[u, qk] = parts_pool.tile([P, HEADS, ROWS, 2 * DH], F32, name="part")
+                mine = part[u, qk][:, :, r, :]
             for h in range(HEADS):
                 nc.vector.scalar_tensor_tensor(
-                    out=part[u, qk][:, h, r, :].rearrange("p (n i) -> p n i", i=2),
+                    out=mine[:, h, :].rearrange("p (n i) -> p n i", i=2),
                     in0=y_bank[slot][:, h * DH : (h + 1) * DH].unsqueeze(2).to_broadcast([P, DH, 2]),
                     scalar=rinv[slot][:, h : h + 1],
                     in1=coef[g, r, qk][:].rearrange("p (n i) -> p n i", i=2),
@@ -314,9 +324,17 @@ def tile_fluxjointattention_pa_t_kernel(
                 op=ALU.add,
             )
 
+        def add_last(slot, eng):
+            u, qk, r = where(slot)
+            if r == 0:
+                res[u, qk] = work.tile([P, HEADS, ROWS, DH], F32, name="res_%d" % qk)
+            eng.tensor_tensor(
+                out=res[u, qk][:, :, r, :], in0=part[slot][:, :, 0, 0:DH], in1=part[slot][:, :, 0, DH:], op=ALU.add
+            )
+
         def t_v(u, r):
             s = place(u)[2]
-            v_bank[u, r] = v_psum.tile([P, BLOCK], F32, name="v_bank")
+            v_bank[u, r] = turn_psum.tile([P, BLOCK], F32, name="turned")
             for again in range(VALUE_PASSES):
                 nc.tensor.matmul_mx(
                     out=v_bank[u, r][:],
@@ -350,76 +368,112 @@ def tile_fluxjointattention_pa_t_kernel(
         w_copy = {}
         w_quant = {}
         for k in range(6):
-            w_turn.setdefault(k - 6, []).append((0, k, k < 4))
-            w_copy.setdefault(k - 6, []).append((0, k, k % 2 == 0))
-            if k != 4:
-                w_quant.setdefault(k - 6, []).append((0, min(k, 4)))
             at = (5, 6, 7, 9, 10, 11)[k]
-            w_turn.setdefault(at, []).append((1, k, False))
-            w_copy.setdefault(at + 1, []).append((1, k, k % 2 == 1))
+            w_turn[at] = (1, k)
+            w_copy[at + 1] = (1, k, k % 2 == 1)
             if k != 4:
-                w_quant.setdefault(at + 2, []).append((1, min(k, 4)))
+                w_quant[at + 2] = (1, min(k, 4))
+        w_turn[0] = (0, 4)
+        w_copy[1] = (0, 4, True)
+        w_turn[1] = (0, 5)
+        w_copy[2] = (0, 5, False)
+        w_quant[3] = (0, 4)
         tables = {}
         later = [(1, r, qk) for qk in range(2) for r in range(ROWS)] + [None]
         later += [(g, r, qk) for g in range(2, GROUPS) for qk in range(2) for r in range(ROWS)]
         for n, what in enumerate(later):
             tables[2 + 3 * n] = what
 
+        values_at = {}
+        for n in range(2 * UNITS):
+            values_at[5 + (7 * n) // 4] = n
+
         for qk in range(2):
             for r in range(ROWS):
                 table_coef(0, r, qk)
         table_v_bias(0)
+        t_in(0)
+        c_in(0)
+        t_w(0, 0, back_psum, "y")
+        c_w(0, 0, True)
+        v_quant(0)
+        t_w(0, 1, back_psum, "y")
+        c_w(0, 1, False)
+        q_w(0, 0)
+        t_w(0, 2, back_psum, "y")
+        c_w(0, 2, False)
+        q_w(0, 1)
+        t_qk(0, 0)
+        evac(0, 0, 0, False)
+        evac(0, 0, 1, False)
+        q_w(0, 2)
+        t_w(0, 3, back_psum, "y")
+        t_qk(0, 1)
+        evac(0, 1, 0, True)
+        evac(0, 1, 1, True)
+        c_w(0, 3, True)
+        t_in(1)
+        c_in(1)
+        t_back(0)
+        t_qk(0, 2)
+        evac(0, 2, 0, False)
+        evac(0, 2, 1, False)
+        v_quant(1)
+        q_w(0, 3)
+        t_qk(0, 3)
+        evac(0, 3, 0, True)
+        evac(0, 3, 1, True)
 
-        for slot in range(-8, SLOTS + 2):
+        for slot in range(0, SLOTS + 1):
             u, i = divmod(slot, 4)
-            live = 0 <= slot < SLOTS
-            ahead = 0 <= u + 1 < UNITS
-            far = 0 <= u + 2 < UNITS
+            live = slot < SLOTS
+            ahead = u + 1 < UNITS
+            far = u + 2 < UNITS
+            done = slot - 1
             if ahead:
                 t_qk(u + 1, i)
-            if 0 <= slot + 1 < SLOTS:
+            if slot + 1 < SLOTS:
                 t_back(slot + 1)
             if i == 0 and far:
                 t_in(u + 2)
-            for s, k, in_back in w_turn.get(slot, []):
-                if in_back:
-                    t_w(s, k, back_psum, "y")
-                else:
-                    t_w(s, k, turn_psum, "turned")
-            if live and i % 2 == 0:
-                t_v(u, i // 2)
+            if slot in w_turn:
+                t_w(w_turn[slot][0], w_turn[slot][1], turn_psum, "turned")
+            if slot + 1 in values_at:
+                t_v(values_at[slot + 1] // 2, values_at[slot + 1] % 2)
             if live:
                 s_squares(slot)
             if ahead:
-                s_evac(u + 1, i, 0)
+                evac(u + 1, i, 0, False)
             if live:
                 s_rinv(slot)
             if ahead:
-                s_evac(u + 1, i, 1)
+                evac(u + 1, i, 1, False)
             if i == 1 and far:
                 c_in(u + 2)
-            for s, k, on_vector in w_copy.get(slot, []):
-                if not on_vector:
-                    c_w(s, k, False)
-            if 0 <= slot - 1 < SLOTS:
-                v_part(slot - 1)
-            if live and i % 2 == 1:
-                v_values(u, i // 2)
+            if slot in w_copy and not w_copy[slot][2]:
+                c_w(w_copy[slot][0], w_copy[slot][1], False)
+            if 0 <= done < SLOTS:
+                v_part(done)
+            if SLOTS - 2 <= done < SLOTS:
+                add_last(done, nc.vector)
+            if slot in values_at:
+                v_values(values_at[slot] // 2, values_at[slot] % 2)
             if i == 2 and far:
                 v_quant(u + 2)
-            for s, k, on_vector in w_copy.get(slot, []):
-                if on_vector:
-                    c_w(s, k, True)
-            for s, piece in w_quant.get(slot, []):
-                q_w(s, piece)
-            if 0 <= slot - 1 < SLOTS and (slot - 1) % 2 == 1:
-                g_add((slot - 1) // 4, ((slot - 1) % 4) // 2)
+            if slot in w_copy and w_copy[slot][2]:
+                c_w(w_copy[slot][0], w_copy[slot][1], True)
+            if slot in w_quant:
+                q_w(w_quant[slot][0], w_quant[slot][1])
+            if 0 <= done < SLOTS - 4 and done % 2 == 1:
+                g_add(done // 4, (done % 4) // 2)
+            if SLOTS - 4 <= done < SLOTS - 2:
+                add_last(done, nc.gpsimd)
             if slot in tables:
                 if tables[slot] is None:
                     table_v_bias(1)
                 else:
                     table_coef(tables[slot][0], tables[slot][1], tables[slot][2])
-            if 0 <= slot - 1 < SLOTS and (slot - 1) % 2 == 1:
-                store((slot - 1) // 4, ((slot - 1) % 4) // 2)
-            if live and i == 3:
-                store(u, 2)
+            if 0 <= done < SLOTS and done % 2 == 1:
+                store(done // 4, (done % 4) // 2)
+            if slot in values_at and values_at[slot] % 2 == 1:
+                store(values_at[slot] // 2, 2)

@@ -79,23 +79,21 @@ def tile_fluxjointattention_pa_t_kernel(
         nc.gpsimd.tensor_copy(
             out=pairs_apart[:].rearrange("p (c j) -> p c j", c=2), in_=ident[:].rearrange("p (j c) -> p c j", c=2)
         )
+        ident_bf = keep.tile([P, P], BF16)
+        make_identity(nc, ident_bf[:])
         eps = keep.tile([P, 1], F32)
         nc.vector.memset(eps[:], EPS)
         bias_rows = keep.tile([P, P], BF16)
         nc.vector.memset(bias_rows[:], 0.0)
+        gain_rows = {}
+        for s in range(2):
+            gain_rows[s] = keep.tile([P, P], BF16, name="gain_rows_%d" % s)
+            nc.vector.memset(gain_rows[s][:], 0.0)
 
-        gain_raw = {}
-        v_bias_raw = {}
         for s in range(2):
             nc.scalar.dma_start(
                 out=bias_rows[s * VECTORS : (s + 1) * VECTORS, :], in_=biases[s].rearrange("(m n) -> m n", n=DH)
             )
-        for s in range(2):
-            for qk in range(2):
-                gain_raw[s, qk] = keep.tile([P, DH], BF16, name="gain_raw_%d_%d" % (s, qk))
-            v_bias_raw[s] = keep.tile([P, BLOCK], BF16, name="v_bias_raw_%d" % s)
-        for qk in range(2):
-            nc.scalar.dma_start(out=gain_raw[0, qk][:], in_=gains[0][qk].partition_broadcast(P))
         warm = keep.tile([P, 1], F32)
         nc.scalar.activation(out=warm[:], in_=eps[:], func=ACT.Abs_reciprocal_sqrt)
 
@@ -127,7 +125,12 @@ def tile_fluxjointattention_pa_t_kernel(
             )
             rope_raw[g] = rows
 
+        def load_gains(s):
+            for qk in range(2):
+                nc.sync.dma_start(out=gain_rows[s][qk : qk + 1, :], in_=gains[s][qk].rearrange("(o n) -> o n", o=1))
+
         load_tokens(0)
+        load_gains(0)
         load_weights(0, 0)
         load_weights(0, 1)
         load_rope(0)
@@ -136,15 +139,12 @@ def tile_fluxjointattention_pa_t_kernel(
         load_tokens(1)
         load_weights(0, 4)
         load_weights(0, 5)
-        nc.sync.dma_start(out=v_bias_raw[0][:], in_=biases[0][2 * BLOCK :].partition_broadcast(P))
+        load_gains(1)
         load_tokens(2)
-        for qk in range(2):
-            nc.sync.dma_start(out=gain_raw[1, qk][:], in_=gains[1][qk].partition_broadcast(P))
         load_rope(1)
         load_tokens(3)
         for k in range(6):
             load_weights(1, k)
-        nc.sync.dma_start(out=v_bias_raw[1][:], in_=biases[1][2 * BLOCK :].partition_broadcast(P))
         load_tokens(4)
         load_tokens(5)
         load_rope(2)
@@ -162,9 +162,28 @@ def tile_fluxjointattention_pa_t_kernel(
         v_bias = {}
         coef = {}
 
-        def table_v_bias(s):
-            v_bias[s] = keep.tile([P, BLOCK], F32, name="v_bias_%d" % s)
-            nc.gpsimd.tensor_copy(out=v_bias[s][:], in_=v_bias_raw[s][:])
+        gain = {}
+        spread = {}
+
+        def t_spread(what, s):
+            rows, first, count = (gain_rows[s], 0, 2) if what == "gain" else (bias_rows, s * VECTORS + 2 * HEADS, HEADS)
+            spread[what, s] = turn_psum.tile([P, count, DH], F32, name="turned")
+            for n in range(count):
+                nc.tensor.matmul(
+                    out=spread[what, s][:, n, :],
+                    lhsT=ident_bf[:, first + n : first + n + 1].to_broadcast([P, P]),
+                    rhs=rows[:],
+                    start=True,
+                    stop=True,
+                )
+
+        def c_spread(what, s):
+            kept = keep.tile([P, 2 if what == "gain" else HEADS, DH], F32, name="%s_%d" % (what, s))
+            nc.scalar.copy(out=kept[:], in_=spread[what, s][:])
+            if what == "gain":
+                gain[s] = kept
+            else:
+                v_bias[s] = kept
 
         def table_coef(g, r, qk):
             s = 0 if g == 0 else 1
@@ -172,7 +191,7 @@ def tile_fluxjointattention_pa_t_kernel(
             nc.gpsimd.tensor_tensor(
                 out=coef[g, r, qk][:].rearrange("p (c j i) -> p c j i", c=2, i=2),
                 in0=rope_raw[g][:, r, :].rearrange("p (j i c) -> p c j i", i=2, c=2),
-                in1=gain_raw[s, qk][:].rearrange("p (j c) -> p c j", c=2).unsqueeze(3).to_broadcast([P, 2, PAIRS, 2]),
+                in1=gain[s][:, qk, :].rearrange("p (j c) -> p c j", c=2).unsqueeze(3).to_broadcast([P, 2, PAIRS, 2]),
                 op=ALU.mult,
             )
 
@@ -353,7 +372,7 @@ def tile_fluxjointattention_pa_t_kernel(
             nc.vector.tensor_tensor(
                 out=res[u, 2][:, :, r, :],
                 in0=v_bank[u, r][:].rearrange("p (h d) -> p h d", h=HEADS),
-                in1=v_bias[s][:].rearrange("p (h d) -> p h d", h=HEADS),
+                in1=v_bias[s][:],
                 op=ALU.add,
             )
 
@@ -378,22 +397,23 @@ def tile_fluxjointattention_pa_t_kernel(
         w_turn[1] = (0, 5)
         w_copy[2] = (0, 5, False)
         w_quant[3] = (0, 4)
+        spread_at = {1: ("gain", 1), 2: ("v_bias", 0), 3: ("v_bias", 1)}
         tables = {}
-        later = [(1, r, qk) for qk in range(2) for r in range(ROWS)] + [None]
-        later += [(g, r, qk) for g in range(2, GROUPS) for qk in range(2) for r in range(ROWS)]
+        later = [(g, r, qk) for g in range(1, GROUPS) for qk in range(2) for r in range(ROWS)]
         for n, what in enumerate(later):
-            tables[2 + 3 * n] = what
+            tables[3 + 3 * n] = what
 
         values_at = {}
         for n in range(2 * UNITS):
             values_at[5 + (7 * n) // 4] = n
 
+        t_in(0)
+        c_in(0)
+        t_spread("gain", 0)
+        c_spread("gain", 0)
         for qk in range(2):
             for r in range(ROWS):
                 table_coef(0, r, qk)
-        table_v_bias(0)
-        t_in(0)
-        c_in(0)
         t_w(0, 0, back_psum, "y")
         c_w(0, 0, True)
         v_quant(0)
@@ -438,6 +458,8 @@ def tile_fluxjointattention_pa_t_kernel(
                 t_in(u + 2)
             if slot in w_turn:
                 t_w(w_turn[slot][0], w_turn[slot][1], turn_psum, "turned")
+            if slot in spread_at:
+                t_spread(spread_at[slot][0], spread_at[slot][1])
             if slot + 1 in values_at:
                 t_v(values_at[slot + 1] // 2, values_at[slot + 1] % 2)
             if live:
@@ -452,6 +474,8 @@ def tile_fluxjointattention_pa_t_kernel(
                 c_in(u + 2)
             if slot in w_copy and not w_copy[slot][2]:
                 c_w(w_copy[slot][0], w_copy[slot][1], False)
+            if slot - 1 in spread_at:
+                c_spread(spread_at[slot - 1][0], spread_at[slot - 1][1])
             if 0 <= done < SLOTS:
                 v_part(done)
             if SLOTS - 2 <= done < SLOTS:
@@ -469,10 +493,7 @@ def tile_fluxjointattention_pa_t_kernel(
             if SLOTS - 4 <= done < SLOTS - 2:
                 add_last(done, nc.gpsimd)
             if slot in tables:
-                if tables[slot] is None:
-                    table_v_bias(1)
-                else:
-                    table_coef(tables[slot][0], tables[slot][1], tables[slot][2])
+                table_coef(tables[slot][0], tables[slot][1], tables[slot][2])
             if 0 <= done < SLOTS and done % 2 == 1:
                 store(done // 4, (done % 4) // 2)
             if slot in values_at and values_at[slot] % 2 == 1:

@@ -110,12 +110,12 @@ def tile_fluxjointattention_pa_t_kernel(
             )
             x_raw[u] = rows
 
-        def load_weights(s, k):
-            rows = keep.tile([P, 2, K], BF16, name="w_raw_%d_%d" % (s, k))
+        def load_weights(s, blk):
+            rows = keep.tile([P, HEADS, K], BF16, name="w_raw_%d_%d" % (s, blk))
             nc.sync.dma_start(
-                out=rows[:], in_=weights[s][2 * k * DH : 2 * (k + 1) * DH, :].rearrange("(h p) k -> p h k", p=P)
+                out=rows[:], in_=weights[s][blk * BLOCK : (blk + 1) * BLOCK, :].rearrange("(h p) k -> p h k", p=P)
             )
-            w_raw[s, k] = rows
+            w_raw[s, blk] = rows
 
         def load_rope(g):
             rows = keep.tile([P, ROWS, PACK * PAIRS], BF16, name="rope_raw_%d" % g)
@@ -132,19 +132,16 @@ def tile_fluxjointattention_pa_t_kernel(
         load_tokens(0)
         load_gains(0)
         load_weights(0, 0)
-        load_weights(0, 1)
         load_rope(0)
-        load_weights(0, 2)
-        load_weights(0, 3)
+        load_weights(0, 1)
         load_tokens(1)
-        load_weights(0, 4)
-        load_weights(0, 5)
+        load_weights(0, 2)
         load_gains(1)
         load_tokens(2)
         load_rope(1)
         load_tokens(3)
-        for k in range(6):
-            load_weights(1, k)
+        for blk in range(3):
+            load_weights(1, blk)
         load_tokens(4)
         load_tokens(5)
         load_rope(2)
@@ -185,10 +182,10 @@ def tile_fluxjointattention_pa_t_kernel(
             else:
                 v_bias[s] = kept
 
-        def table_coef(g, r, qk):
+        def table_coef(g, r, qk, eng):
             s = 0 if g == 0 else 1
             coef[g, r, qk] = keep.tile([P, 2 * DH], F32, name="coef_%d_%d_%d" % (g, r, qk))
-            nc.gpsimd.tensor_tensor(
+            eng.tensor_tensor(
                 out=coef[g, r, qk][:].rearrange("p (c j i) -> p c j i", c=2, i=2),
                 in0=rope_raw[g][:, r, :].rearrange("p (j i c) -> p c j i", i=2, c=2),
                 in1=gain[s][:, qk, :].rearrange("p (j c) -> p c j", c=2).unsqueeze(3).to_broadcast([P, 2, PAIRS, 2]),
@@ -239,7 +236,7 @@ def tile_fluxjointattention_pa_t_kernel(
             nc.vector.quantize_mx(out=x_codes[u][:].bitcast(FP8X4), scales=x_scales[u][:], in_=grouped_x[u][:])
 
         def t_w(s, k, pool, tag):
-            turned_w[s, k] = turn(pool, tag, lambda t: w_raw[s, k][:, t, :].bitcast(F32))
+            turned_w[s, k] = turn(pool, tag, lambda t: w_raw[s, k // 2][:, 2 * (k % 2) + t, :].bitcast(F32))
 
         def c_w(s, k, on_vector):
             piece = min(k, 4)
@@ -401,7 +398,7 @@ def tile_fluxjointattention_pa_t_kernel(
         tables = {}
         later = [(g, r, qk) for g in range(1, GROUPS) for qk in range(2) for r in range(ROWS)]
         for n, what in enumerate(later):
-            tables[3 + 3 * n] = what
+            tables[2 + 4 * n] = what
 
         values_at = {}
         for n in range(2 * UNITS):
@@ -411,9 +408,6 @@ def tile_fluxjointattention_pa_t_kernel(
         c_in(0)
         t_spread("gain", 0)
         c_spread("gain", 0)
-        for qk in range(2):
-            for r in range(ROWS):
-                table_coef(0, r, qk)
         t_w(0, 0, back_psum, "y")
         c_w(0, 0, True)
         v_quant(0)
@@ -423,6 +417,8 @@ def tile_fluxjointattention_pa_t_kernel(
         t_w(0, 2, back_psum, "y")
         c_w(0, 2, False)
         q_w(0, 1)
+        table_coef(0, 0, 0, nc.vector)
+        table_coef(0, 1, 0, nc.vector)
         t_qk(0, 0)
         evac(0, 0, 0, False)
         evac(0, 0, 1, False)
@@ -440,6 +436,8 @@ def tile_fluxjointattention_pa_t_kernel(
         evac(0, 2, 1, False)
         v_quant(1)
         q_w(0, 3)
+        table_coef(0, 0, 1, nc.vector)
+        table_coef(0, 1, 1, nc.vector)
         t_qk(0, 3)
         evac(0, 3, 0, True)
         evac(0, 3, 1, True)
@@ -478,22 +476,22 @@ def tile_fluxjointattention_pa_t_kernel(
                 c_spread(spread_at[slot - 1][0], spread_at[slot - 1][1])
             if 0 <= done < SLOTS:
                 v_part(done)
+            if i == 2 and far:
+                v_quant(u + 2)
+            if slot in w_quant:
+                q_w(w_quant[slot][0], w_quant[slot][1])
             if SLOTS - 2 <= done < SLOTS:
                 add_last(done, nc.vector)
             if slot in values_at:
                 v_values(values_at[slot] // 2, values_at[slot] % 2)
-            if i == 2 and far:
-                v_quant(u + 2)
             if slot in w_copy and w_copy[slot][2]:
                 c_w(w_copy[slot][0], w_copy[slot][1], True)
-            if slot in w_quant:
-                q_w(w_quant[slot][0], w_quant[slot][1])
             if 0 <= done < SLOTS - 4 and done % 2 == 1:
                 g_add(done // 4, (done % 4) // 2)
             if SLOTS - 4 <= done < SLOTS - 2:
                 add_last(done, nc.gpsimd)
             if slot in tables:
-                table_coef(tables[slot][0], tables[slot][1], tables[slot][2])
+                table_coef(tables[slot][0], tables[slot][1], tables[slot][2], nc.gpsimd)
             if 0 <= done < SLOTS and done % 2 == 1:
                 store(done // 4, (done % 4) // 2)
             if slot in values_at and values_at[slot] % 2 == 1:

@@ -176,7 +176,10 @@ def tile_fluxjointattention_pa_t_kernel(
 
         def c_spread(what, s):
             kept = keep.tile([P, 2 if what == "gain" else HEADS, DH], F32, name="%s_%d" % (what, s))
-            nc.scalar.copy(out=kept[:], in_=spread[what, s][:])
+            if what == "gain":
+                nc.scalar.copy(out=kept[:], in_=spread[what, s][:])
+            else:
+                nc.vector.tensor_copy(out=kept[:], in_=spread[what, s][:])
             if what == "gain":
                 gain[s] = kept
             else:
@@ -198,8 +201,7 @@ def tile_fluxjointattention_pa_t_kernel(
         x_scales = {}
         turned_w = {}
         grouped_w = {}
-        w_codes = {}
-        w_scales = {}
+        w_view = {}
         qk_bank = {}
         y_turned = {}
         y_bank = {}
@@ -238,22 +240,34 @@ def tile_fluxjointattention_pa_t_kernel(
         def t_w(s, k, pool, tag):
             turned_w[s, k] = turn(pool, tag, lambda t: w_raw[s, k // 2][:, 2 * (k % 2) + t, :].bitcast(F32))
 
+        def by_block(s, k):
+            return s == 1 or k >= 4
+
         def c_w(s, k, on_vector):
-            piece = min(k, 4)
-            if k <= 4:
-                width = 2 * DH if k < 4 else BLOCK
-                grouped_w[s, piece] = stage.tile([P, width * PACK], BF16, align_bytes=64, name="w_grouped")
-            words = grouped_w[s, piece][:].bitcast(F32).rearrange("p (h n u) -> p h n u", n=DH, u=HALVES)
-            first = 2 * (k - piece)
+            if by_block(s, k):
+                key, first = (s, "block", k // 2), 2 * (k % 2)
+            else:
+                key, first = (s, "step", k), 0
+            if first == 0:
+                width = BLOCK if by_block(s, k) else 2 * DH
+                grouped_w[key] = stage.tile([P, width * PACK], BF16, align_bytes=64, name="w_grouped")
+            words = grouped_w[key][:].bitcast(F32).rearrange("p (h n u) -> p h n u", n=DH, u=HALVES)
             group(on_vector, turned_w[s, k], words[:, first : first + 2])
 
-        def q_w(s, piece):
-            width = 2 * DH if piece < 4 else BLOCK
-            w_codes[s, piece] = keep.tile([P, width], U32, align_bytes=64, name="w_codes_%d_%d" % (s, piece))
-            w_scales[s, piece] = keep.tile([P, width], U8, align_bytes=64, name="w_scales_%d_%d" % (s, piece))
-            nc.vector.quantize_mx(
-                out=w_codes[s, piece][:].bitcast(FP8X4), scales=w_scales[s, piece][:], in_=grouped_w[s, piece][:]
-            )
+        def q_w(s, k):
+            key = (s, "block", k // 2) if by_block(s, k) else (s, "step", k)
+            width = BLOCK if by_block(s, k) else 2 * DH
+            codes = keep.tile([P, width], U32, align_bytes=64, name="w_codes_%d_%d" % (s, k))
+            scales = keep.tile([P, width], U8, align_bytes=64, name="w_scales_%d_%d" % (s, k))
+            nc.vector.quantize_mx(out=codes[:].bitcast(FP8X4), scales=scales[:], in_=grouped_w[key][:])
+            if k >= 4:
+                w_view[s, 4] = (codes[:], scales[:])
+            elif by_block(s, k):
+                for half in range(2):
+                    cols = slice(half * 2 * DH, (half + 1) * 2 * DH)
+                    w_view[s, k - 1 + half] = (codes[:, cols], scales[:, cols])
+            else:
+                w_view[s, k] = (codes[:], scales[:])
 
         def t_qk(u, j):
             s = place(u)[2]
@@ -261,8 +275,8 @@ def tile_fluxjointattention_pa_t_kernel(
             for t in [t for again in range(QK_PASSES) for t in range(2)]:
                 nc.tensor.matmul_mx(
                     out=qk_bank[u, j][:, t, :],
-                    lhsT=w_codes[s, j][:, t * DH : (t + 1) * DH].bitcast(FP8X4),
-                    lhsT_scale=w_scales[s, j][:, t * DH : (t + 1) * DH],
+                    lhsT=w_view[s, j][0][:, t * DH : (t + 1) * DH].bitcast(FP8X4),
+                    lhsT_scale=w_view[s, j][1][:, t * DH : (t + 1) * DH],
                     rhs=x_codes[u][:].bitcast(FP8X4),
                     rhs_scale=x_scales[u][:],
                     start=True,
@@ -356,8 +370,8 @@ def tile_fluxjointattention_pa_t_kernel(
                     out=v_bank[u, r][:],
                     lhsT=x_codes[u][:, r * P : (r + 1) * P].bitcast(FP8X4),
                     lhsT_scale=x_scales[u][:, r * P : (r + 1) * P],
-                    rhs=w_codes[s, 4][:].bitcast(FP8X4),
-                    rhs_scale=w_scales[s, 4][:],
+                    rhs=w_view[s, 4][0].bitcast(FP8X4),
+                    rhs_scale=w_view[s, 4][1],
                     start=True,
                     stop=True,
                 )
@@ -384,25 +398,25 @@ def tile_fluxjointattention_pa_t_kernel(
         w_copy = {}
         w_quant = {}
         for k in range(6):
-            at = (5, 6, 7, 9, 10, 11)[k]
+            at = (5, 6, 9, 10, 13, 14)[k]
             w_turn[at] = (1, k)
             w_copy[at + 1] = (1, k, k % 2 == 1)
-            if k != 4:
-                w_quant[at + 2] = (1, min(k, 4))
+            if k % 2 == 1:
+                w_quant[at + 2] = (1, k)
         w_turn[0] = (0, 4)
         w_copy[1] = (0, 4, True)
         w_turn[1] = (0, 5)
         w_copy[2] = (0, 5, False)
-        w_quant[3] = (0, 4)
-        spread_at = {1: ("gain", 1), 2: ("v_bias", 0), 3: ("v_bias", 1)}
+        w_quant[4] = (0, 5)
+        spread_at = {-1: ("gain", 1), 2: ("v_bias", 0), 3: ("v_bias", 1)}
         tables = {}
         later = [(g, r, qk) for g in range(1, GROUPS) for qk in range(2) for r in range(ROWS)]
         for n, what in enumerate(later):
-            tables[2 + 4 * n] = what
+            tables.setdefault(n // 2 if n < 4 else 2 + 4 * n, []).append(what)
 
         values_at = {}
         for n in range(2 * UNITS):
-            values_at[5 + (7 * n) // 4] = n
+            values_at[6 + (7 * n) // 4] = n
 
         t_in(0)
         c_in(0)
@@ -441,6 +455,7 @@ def tile_fluxjointattention_pa_t_kernel(
         t_qk(0, 3)
         evac(0, 3, 0, True)
         evac(0, 3, 1, True)
+        t_spread("gain", 1)
 
         for slot in range(0, SLOTS + 1):
             u, i = divmod(slot, 4)
@@ -466,7 +481,7 @@ def tile_fluxjointattention_pa_t_kernel(
                 evac(u + 1, i, 0, False)
             if live:
                 s_rinv(slot)
-            if ahead:
+            if ahead and not (i == 1 and u % 2 == 1):
                 evac(u + 1, i, 1, False)
             if i == 1 and far:
                 c_in(u + 2)
@@ -480,8 +495,11 @@ def tile_fluxjointattention_pa_t_kernel(
                 v_quant(u + 2)
             if slot in w_quant:
                 q_w(w_quant[slot][0], w_quant[slot][1])
-            if SLOTS - 2 <= done < SLOTS:
+            if done == SLOTS - 1:
+                add_last(done - 1, nc.vector)
                 add_last(done, nc.vector)
+            if ahead and i == 1 and u % 2 == 1:
+                evac(u + 1, i, 1, True)
             if slot in values_at:
                 v_values(values_at[slot] // 2, values_at[slot] % 2)
             if slot in w_copy and w_copy[slot][2]:
@@ -490,8 +508,8 @@ def tile_fluxjointattention_pa_t_kernel(
                 g_add(done // 4, (done % 4) // 2)
             if SLOTS - 4 <= done < SLOTS - 2:
                 add_last(done, nc.gpsimd)
-            if slot in tables:
-                table_coef(tables[slot][0], tables[slot][1], tables[slot][2], nc.gpsimd)
+            for g, r, qk in tables.get(slot, []):
+                table_coef(g, r, qk, nc.gpsimd)
             if 0 <= done < SLOTS and done % 2 == 1:
                 store(done // 4, (done % 4) // 2)
             if slot in values_at and values_at[slot] % 2 == 1:

@@ -151,10 +151,6 @@ def tile_fluxjointattention_pa_t_kernel(
 
         bias_cols = keep.tile([P, P], F32)
         bias_rows_f32 = keep.tile([P, P], F32)
-        nc.vector.tensor_copy(out=bias_rows_f32[:], in_=bias_rows[:])
-        bias_turned = turn_psum.tile([P, P], F32, name="turned")
-        nc.tensor.transpose(bias_turned[:], bias_rows_f32[:], ident[:])
-        nc.vector.tensor_copy(out=bias_cols[:], in_=bias_turned[:])
 
         v_bias = {}
         coef = {}
@@ -176,10 +172,7 @@ def tile_fluxjointattention_pa_t_kernel(
 
         def c_spread(what, s):
             kept = keep.tile([P, 2 if what == "gain" else HEADS, DH], F32, name="%s_%d" % (what, s))
-            if what == "gain":
-                nc.scalar.copy(out=kept[:], in_=spread[what, s][:])
-            else:
-                nc.vector.tensor_copy(out=kept[:], in_=spread[what, s][:])
+            nc.scalar.copy(out=kept[:], in_=spread[what, s][:])
             if what == "gain":
                 gain[s] = kept
             else:
@@ -431,8 +424,12 @@ def tile_fluxjointattention_pa_t_kernel(
         t_w(0, 2, back_psum, "y")
         c_w(0, 2, False)
         q_w(0, 1)
+        nc.vector.tensor_copy(out=bias_rows_f32[:], in_=bias_rows[:])
+        bias_turned = turn_psum.tile([P, P], F32, name="turned")
+        nc.tensor.transpose(bias_turned[:], bias_rows_f32[:], ident[:])
         table_coef(0, 0, 0, nc.vector)
         table_coef(0, 1, 0, nc.vector)
+        nc.vector.tensor_copy(out=bias_cols[:], in_=bias_turned[:])
         t_qk(0, 0)
         evac(0, 0, 0, False)
         evac(0, 0, 1, False)
@@ -481,7 +478,7 @@ def tile_fluxjointattention_pa_t_kernel(
                 evac(u + 1, i, 0, False)
             if live:
                 s_rinv(slot)
-            if ahead and not (i == 1 and u % 2 == 1):
+            if ahead:
                 evac(u + 1, i, 1, False)
             if i == 1 and far:
                 c_in(u + 2)
@@ -498,8 +495,6 @@ def tile_fluxjointattention_pa_t_kernel(
             if done == SLOTS - 1:
                 add_last(done - 1, nc.vector)
                 add_last(done, nc.vector)
-            if ahead and i == 1 and u % 2 == 1:
-                evac(u + 1, i, 1, True)
             if slot in values_at:
                 v_values(values_at[slot] // 2, values_at[slot] % 2)
             if slot in w_copy and w_copy[slot][2]:

from contextlib import ExitStack

import concourse.mybir as mybir
from concourse.masks import make_identity

F32 = mybir.dt.float32
BF16 = mybir.dt.bfloat16
U32 = mybir.dt.uint32
U8 = mybir.dt.uint8
FP8X4 = mybir.dt.float8_e4m3fn_x4
ACT = mybir.ActivationFunctionType
ALU = mybir.AluOpType

P = 128
BATCH = 4
HEADS = 4
DH = 128
PAIRS = DH // 2
K = 512
PACK = 4
HALVES = 2
BLOCK = HEADS * DH
VECTORS = 3 * HEADS
ROWS = 2
UNIT = P * ROWS
GROUPS = 1024 // UNIT
UNITS = GROUPS * BATCH
SLOTS = 4 * UNITS
EPS = 1e-6
VALUE_PASSES = 1
QK_PASSES = 1

FLOPS = 2 * BATCH * 1024 * K * 3 * BLOCK


def tile_fluxjointattention_pa_t_kernel(
    tc,
    hidden_states_a,
    hidden_states_b,
    image_rotary_emb,
    a_qkv_w,
    a_qkv_b,
    b_qkv_w,
    b_qkv_b,
    norm_q_a_w,
    norm_k_a_w,
    norm_q_b_w,
    norm_k_b_w,
    out_0,
    out_1,
    out_2,
):
    nc = tc.nc
    outs = (out_0, out_1, out_2)
    hidden = (hidden_states_b, hidden_states_a)
    weights = (b_qkv_w, a_qkv_w)
    biases = (b_qkv_b, a_qkv_b)
    gains = ((norm_q_b_w, norm_k_b_w), (norm_q_a_w, norm_k_a_w))

    with ExitStack() as stack:
        keep = stack.enter_context(tc.tile_pool(name="keep", bufs=1))
        stage = stack.enter_context(tc.tile_pool(name="stage", bufs=2))
        codes_pool = stack.enter_context(tc.tile_pool(name="codes_pool", bufs=4))
        work = stack.enter_context(tc.tile_pool(name="work", bufs=3))
        parts_pool = stack.enter_context(tc.tile_pool(name="parts_pool", bufs=4))
        small = stack.enter_context(tc.tile_pool(name="small", bufs=4))
        turn_psum = stack.enter_context(tc.psum_pool(name="turn_psum", bufs=3))
        qk_psum = stack.enter_context(tc.psum_pool(name="qk_psum", bufs=2))
        back_psum = stack.enter_context(tc.psum_pool(name="back_psum", bufs=3))
        stack.enter_context(tc.manual_schedule())

        def place(u):
            g, b = divmod(u, BATCH)
            return g, b, (0 if g == 0 else 1)

        ident = keep.tile([P, P], F32)
        make_identity(nc, ident[:])
        pairs_apart = keep.tile([P, P], F32)
        nc.gpsimd.tensor_copy(
            out=pairs_apart[:].rearrange("p (c j) -> p c j", c=2), in_=ident[:].rearrange("p (j c) -> p c j", c=2)
        )
        ident_bf = keep.tile([P, P], BF16)
        make_identity(nc, ident_bf[:])
        eps = keep.tile([P, 1], F32)
        nc.vector.memset(eps[:], EPS)
        bias_rows = keep.tile([P, P], BF16)
        nc.vector.memset(bias_rows[:], 0.0)
        gain_rows = {}
        for s in range(2):
            gain_rows[s] = keep.tile([P, P], BF16, name="gain_rows_%d" % s)
            nc.vector.memset(gain_rows[s][:], 0.0)

        for s in range(2):
            nc.scalar.dma_start(
                out=bias_rows[s * VECTORS : (s + 1) * VECTORS, :], in_=biases[s].rearrange("(m n) -> m n", n=DH)
            )
        warm = keep.tile([P, 1], F32)
        nc.scalar.activation(out=warm[:], in_=eps[:], func=ACT.Abs_reciprocal_sqrt)

        x_raw = {}
        w_raw = {}
        rope_raw = {}

        def load_tokens(u):
            g, b, s = place(u)
            first = 0 if g == 0 else (g - 1) * UNIT
            rows = keep.tile([P, ROWS, K], BF16, name="x_raw_%d" % u)
            nc.sync.dma_start(
                out=rows[:], in_=hidden[s][b, first : first + UNIT, :].rearrange("(p r) k -> p r k", r=ROWS)
            )
            x_raw[u] = rows

        def load_weights(s, blk):
            rows = keep.tile([P, HEADS, K], BF16, name="w_raw_%d_%d" % (s, blk))
            nc.sync.dma_start(
                out=rows[:], in_=weights[s][blk * BLOCK : (blk + 1) * BLOCK, :].rearrange("(h p) k -> p h k", p=P)
            )
            w_raw[s, blk] = rows

        def load_rope(g):
            rows = keep.tile([P, ROWS, PACK * PAIRS], BF16, name="rope_raw_%d" % g)
            nc.sync.dma_start(
                out=rows[:],
                in_=image_rotary_emb[0, 0, g * UNIT : (g + 1) * UNIT].rearrange("(p r) j i c -> p r (j i c)", r=ROWS),
            )
            rope_raw[g] = rows

        def load_gains(s):
            for qk in range(2):
                nc.sync.dma_start(out=gain_rows[s][qk : qk + 1, :], in_=gains[s][qk].rearrange("(o n) -> o n", o=1))

        load_tokens(0)
        load_gains(0)
        load_weights(0, 0)
        load_rope(0)
        load_weights(0, 1)
        load_tokens(1)
        load_weights(0, 2)
        load_gains(1)
        load_tokens(2)
        load_rope(1)
        load_tokens(3)
        for blk in range(3):
            load_weights(1, blk)
        load_tokens(4)
        load_tokens(5)
        load_rope(2)
        load_rope(3)
        for u in range(6, UNITS):
            load_tokens(u)

        bias_cols = keep.tile([P, P], F32)
        bias_rows_f32 = keep.tile([P, P], F32)

        v_bias = {}
        coef = {}

        gain = {}
        spread = {}

        def t_spread(what, s):
            rows, first, count = (gain_rows[s], 0, 2) if what == "gain" else (bias_rows, s * VECTORS + 2 * HEADS, HEADS)
            spread[what, s] = turn_psum.tile([P, count, DH], F32, name="turned")
            for n in range(count):
                nc.tensor.matmul(
                    out=spread[what, s][:, n, :],
                    lhsT=ident_bf[:, first + n : first + n + 1].to_broadcast([P, P]),
                    rhs=rows[:],
                    start=True,
                    stop=True,
                )

        def c_spread(what, s):
            kept = keep.tile([P, 2 if what == "gain" else HEADS, DH], F32, name="%s_%d" % (what, s))
            nc.scalar.copy(out=kept[:], in_=spread[what, s][:])
            if what == "gain":
                gain[s] = kept
            else:
                v_bias[s] = kept

        def table_coef(g, r, qk, eng):
            s = 0 if g == 0 else 1
            coef[g, r, qk] = keep.tile([P, 2 * DH], F32, name="coef_%d_%d_%d" % (g, r, qk))
            eng.tensor_tensor(
                out=coef[g, r, qk][:].rearrange("p (c j i) -> p c j i", c=2, i=2),
                in0=rope_raw[g][:, r, :].rearrange("p (j i c) -> p c j i", i=2, c=2),
                in1=gain[s][:, qk, :].rearrange("p (j c) -> p c j", c=2).unsqueeze(3).to_broadcast([P, 2, PAIRS, 2]),
                op=ALU.mult,
            )

        turned_x = {}
        grouped_x = {}
        x_codes = {}
        x_scales = {}
        turned_w = {}
        grouped_w = {}
        w_view = {}
        qk_bank = {}
        y_turned = {}
        y_bank = {}
        sumsq = {}
        rinv = {}
        part = {}
        res = {}
        v_bank = {}

        def turn(pool, tag, raw_rows):
            turned = pool.tile([P, 2, HALVES, P], F32, name=tag)
            for t in range(2):
                for v in range(HALVES):
                    nc.tensor.transpose(turned[:, t, v, :], raw_rows(t)[:, v * P : (v + 1) * P], ident[:])
            return turned

        def group(on_vector, turned, words):
            src = turned[:].rearrange("p t u n -> p t n u")
            if on_vector:
                nc.vector.tensor_copy(out=words, in_=src)
            else:
                nc.scalar.copy(out=words, in_=src)

        def t_in(u):
            turned_x[u] = turn(turn_psum, "turned", lambda r: x_raw[u][:, r, :].bitcast(F32))

        def c_in(u):
            grouped_x[u] = stage.tile([P, UNIT * PACK], BF16, align_bytes=64, name="x_grouped")
            group(False, turned_x[u], grouped_x[u][:].bitcast(F32).rearrange("p (r n u) -> p r n u", r=ROWS, u=HALVES))

        def v_quant(u):
            x_codes[u] = codes_pool.tile([P, UNIT], U32, align_bytes=64, name="x_codes")
            x_scales[u] = codes_pool.tile([P, UNIT], U8, align_bytes=64, name="x_scales")
            nc.vector.quantize_mx(out=x_codes[u][:].bitcast(FP8X4), scales=x_scales[u][:], in_=grouped_x[u][:])

        def t_w(s, k, pool, tag):
            turned_w[s, k] = turn(pool, tag, lambda t: w_raw[s, k // 2][:, 2 * (k % 2) + t, :].bitcast(F32))

        def by_block(s, k):
            return s == 1 or k >= 4

        def c_w(s, k, on_vector):
            if by_block(s, k):
                key, first = (s, "block", k // 2), 2 * (k % 2)
            else:
                key, first = (s, "step", k), 0
            if first == 0:
                width = BLOCK if by_block(s, k) else 2 * DH
                grouped_w[key] = stage.tile([P, width * PACK], BF16, align_bytes=64, name="w_grouped")
            words = grouped_w[key][:].bitcast(F32).rearrange("p (h n u) -> p h n u", n=DH, u=HALVES)
            group(on_vector, turned_w[s, k], words[:, first : first + 2])

        def q_w(s, k):
            key = (s, "block", k // 2) if by_block(s, k) else (s, "step", k)
            width = BLOCK if by_block(s, k) else 2 * DH
            codes = keep.tile([P, width], U32, align_bytes=64, name="w_codes_%d_%d" % (s, k))
            scales = keep.tile([P, width], U8, align_bytes=64, name="w_scales_%d_%d" % (s, k))
            nc.vector.quantize_mx(out=codes[:].bitcast(FP8X4), scales=scales[:], in_=grouped_w[key][:])
            if k >= 4:
                w_view[s, 4] = (codes[:], scales[:])
            elif by_block(s, k):
                for half in range(2):
                    cols = slice(half * 2 * DH, (half + 1) * 2 * DH)
                    w_view[s, k - 1 + half] = (codes[:, cols], scales[:, cols])
            else:
                w_view[s, k] = (codes[:], scales[:])

        def t_qk(u, j):
            s = place(u)[2]
            qk_bank[u, j] = qk_psum.tile([P, 2, UNIT], F32, name="qk_bank")
            for t in [t for again in range(QK_PASSES) for t in range(2)]:
                nc.tensor.matmul_mx(
                    out=qk_bank[u, j][:, t, :],
                    lhsT=w_view[s, j][0][:, t * DH : (t + 1) * DH].bitcast(FP8X4),
                    lhsT_scale=w_view[s, j][1][:, t * DH : (t + 1) * DH],
                    rhs=x_codes[u][:].bitcast(FP8X4),
                    rhs_scale=x_scales[u][:],
                    start=True,
                    stop=True,
                )

        def evac(u, j, t, on_vector):
            s = place(u)[2]
            if j == 0 and t == 0:
                y_turned[u] = stage.tile([P, 2 * HEADS, UNIT], F32, name="y_turned")
            m = 2 * j + t
            bias = bias_cols[:, s * VECTORS + m : s * VECTORS + m + 1]
            if on_vector:
                nc.vector.tensor_scalar(
                    out=y_turned[u][:, m, :], in0=qk_bank[u, j][:, t, :], scalar1=bias, scalar2=None, op0=ALU.add
                )
            else:
                nc.scalar.activation(out=y_turned[u][:, m, :], in_=qk_bank[u, j][:, t, :], func=ACT.Identity, bias=bias)

        def where(slot):
            u, i = divmod(slot, 4)
            qk, r = divmod(i, 2)
            return u, qk, r

        def t_back(slot):
            u, qk, r = where(slot)
            y_bank[slot] = back_psum.tile([P, BLOCK], F32, name="y")
            for h in range(HEADS):
                nc.tensor.transpose(
                    y_bank[slot][:, h * DH : (h + 1) * DH], y_turned[u][:, qk * HEADS + h, r * P : (r + 1) * P], pairs_apart[:]
                )

        def s_squares(slot):
            squares = work.tile([P, BLOCK], BF16, name="squares")
            sumsq[slot] = small.tile([P, HEADS], F32, name="sumsq")
            for h in range(HEADS):
                head = slice(h * DH, (h + 1) * DH)
                nc.scalar.activation(
                    out=squares[:, head], in_=y_bank[slot][:, head], func=ACT.Square, accum_out=sumsq[slot][:, h : h + 1]
                )

        def s_rinv(slot):
            rinv[slot] = small.tile([P, HEADS], F32, name="rinv")
            nc.scalar.activation(
                out=rinv[slot][:], in_=sumsq[slot][:], func=ACT.Abs_reciprocal_sqrt, scale=1.0 / DH, bias=eps[:]
            )

        def v_part(slot):
            u, qk, r = where(slot)
            g = place(u)[0]
            if slot >= SLOTS - 4:
                part[slot] = parts_pool.tile([P, HEADS, 1, 2 * DH], F32, name="part")
                mine = part[slot][:, :, 0, :]
            else:
                if r == 0:
                    part[u, qk] = parts_pool.tile([P, HEADS, ROWS, 2 * DH], F32, name="part")
                mine = part[u, qk][:, :, r, :]
            for h in range(HEADS):
                nc.vector.scalar_tensor_tensor(
                    out=mine[:, h, :].rearrange("p (n i) -> p n i", i=2),
                    in0=y_bank[slot][:, h * DH : (h + 1) * DH].unsqueeze(2).to_broadcast([P, DH, 2]),
                    scalar=rinv[slot][:, h : h + 1],
                    in1=coef[g, r, qk][:].rearrange("p (n i) -> p n i", i=2),
                    op0=ALU.mult,
                    op1=ALU.mult,
                )

        def g_add(u, qk):
            res[u, qk] = work.tile([P, HEADS, ROWS, DH], F32, name="res_%d" % qk)
            planes = part[u, qk][:].rearrange("p h r (c n) -> p (h r) c n", c=2)
            nc.gpsimd.tensor_tensor(
                out=res[u, qk][:].rearrange("p h r n -> p (h r) n"),
                in0=planes[:, :, 0, :],
                in1=planes[:, :, 1, :],
                op=ALU.add,
            )

        def add_last(slot, eng):
            u, qk, r = where(slot)
            if r == 0:
                res[u, qk] = work.tile([P, HEADS, ROWS, DH], F32, name="res_%d" % qk)
            eng.tensor_tensor(
                out=res[u, qk][:, :, r, :], in0=part[slot][:, :, 0, 0:DH], in1=part[slot][:, :, 0, DH:], op=ALU.add
            )

        def t_v(u, r):
            s = place(u)[2]
            v_bank[u, r] = turn_psum.tile([P, BLOCK], F32, name="turned")
            for again in range(VALUE_PASSES):
                nc.tensor.matmul_mx(
                    out=v_bank[u, r][:],
                    lhsT=x_codes[u][:, r * P : (r + 1) * P].bitcast(FP8X4),
                    lhsT_scale=x_scales[u][:, r * P : (r + 1) * P],
                    rhs=w_view[s, 4][0].bitcast(FP8X4),
                    rhs_scale=w_view[s, 4][1],
                    start=True,
                    stop=True,
                )

        def v_values(u, r):
            s = place(u)[2]
            if r == 0:
                res[u, 2] = work.tile([P, HEADS, ROWS, DH], F32, name="res_2")
            nc.vector.tensor_tensor(
                out=res[u, 2][:, :, r, :],
                in0=v_bank[u, r][:].rearrange("p (h d) -> p h d", h=HEADS),
                in1=v_bias[s][:],
                op=ALU.add,
            )

        def store(u, which):
            g, b, s = place(u)
            nc.sync.dma_start(
                out=outs[which][b, :, g * UNIT : (g + 1) * UNIT, :].rearrange("h (p r) d -> p h (r d)", r=ROWS),
                in_=res[u, which][:].rearrange("p h r d -> p h (r d)"),
            )

        w_turn = {}
        w_copy = {}
        w_quant = {}
        for k in range(6):
            at = (5, 6, 9, 10, 13, 14)[k]
            w_turn[at] = (1, k)
            w_copy[at + 1] = (1, k, k % 2 == 1)
            if k % 2 == 1:
                w_quant[at + 2] = (1, k)
        w_turn[0] = (0, 4)
        w_copy[1] = (0, 4, True)
        w_turn[1] = (0, 5)
        w_copy[2] = (0, 5, False)
        w_quant[4] = (0, 5)
        spread_at = {-1: ("gain", 1), 2: ("v_bias", 0), 3: ("v_bias", 1)}
        tables = {}
        later = [(g, r, qk) for g in range(1, GROUPS) for qk in range(2) for r in range(ROWS)]
        for n, what in enumerate(later):
            tables.setdefault(n // 2 if n < 4 else 2 + 4 * n, []).append(what)

        values_at = {}
        for n in range(2 * UNITS):
            values_at[6 + (7 * n) // 4] = n

        t_in(0)
        c_in(0)
        t_spread("gain", 0)
        c_spread("gain", 0)
        t_w(0, 0, back_psum, "y")
        c_w(0, 0, True)
        v_quant(0)
        t_w(0, 1, back_psum, "y")
        c_w(0, 1, False)
        q_w(0, 0)
        t_w(0, 2, back_psum, "y")
        c_w(0, 2, False)
        q_w(0, 1)
        nc.vector.tensor_copy(out=bias_rows_f32[:], in_=bias_rows[:])
        bias_turned = turn_psum.tile([P, P], F32, name="turned")
        nc.tensor.transpose(bias_turned[:], bias_rows_f32[:], ident[:])
        table_coef(0, 0, 0, nc.vector)
        table_coef(0, 1, 0, nc.vector)
        nc.vector.tensor_copy(out=bias_cols[:], in_=bias_turned[:])
        t_qk(0, 0)
        evac(0, 0, 0, False)
        evac(0, 0, 1, False)
        q_w(0, 2)
        t_w(0, 3, back_psum, "y")
        t_qk(0, 1)
        evac(0, 1, 0, True)
        evac(0, 1, 1, True)
        c_w(0, 3, True)
        t_in(1)
        c_in(1)
        t_back(0)
        t_qk(0, 2)
        evac(0, 2, 0, False)
        evac(0, 2, 1, False)
        v_quant(1)
        q_w(0, 3)
        table_coef(0, 0, 1, nc.vector)
        table_coef(0, 1, 1, nc.vector)
        t_qk(0, 3)
        evac(0, 3, 0, True)
        evac(0, 3, 1, True)
        t_spread("gain", 1)

        for slot in range(0, SLOTS + 1):
            u, i = divmod(slot, 4)
            live = slot < SLOTS
            ahead = u + 1 < UNITS
            far = u + 2 < UNITS
            done = slot - 1
            if ahead:
                t_qk(u + 1, i)
            if slot + 1 < SLOTS:
                t_back(slot + 1)
            if i == 0 and far:
                t_in(u + 2)
            if slot in w_turn:
                t_w(w_turn[slot][0], w_turn[slot][1], turn_psum, "turned")
            if slot in spread_at:
                t_spread(spread_at[slot][0], spread_at[slot][1])
            if slot + 1 in values_at:
                t_v(values_at[slot + 1] // 2, values_at[slot + 1] % 2)
            if live:
                s_squares(slot)
            if ahead:
                evac(u + 1, i, 0, False)
            if live:
                s_rinv(slot)
            if ahead:
                evac(u + 1, i, 1, False)
            if i == 1 and far:
                c_in(u + 2)
            if slot in w_copy and not w_copy[slot][2]:
                c_w(w_copy[slot][0], w_copy[slot][1], False)
            if slot - 1 in spread_at:
                c_spread(spread_at[slot - 1][0], spread_at[slot - 1][1])
            if 0 <= done < SLOTS:
                v_part(done)
            if i == 2 and far:
                v_quant(u + 2)
            if slot in w_quant:
                q_w(w_quant[slot][0], w_quant[slot][1])
            if done == SLOTS - 1:
                add_last(done - 1, nc.vector)
                add_last(done, nc.vector)
            if slot in values_at:
                v_values(values_at[slot] // 2, values_at[slot] % 2)
            if slot in w_copy and w_copy[slot][2]:
                c_w(w_copy[slot][0], w_copy[slot][1], True)
            if 0 <= done < SLOTS - 4 and done % 2 == 1:
                g_add(done // 4, (done % 4) // 2)
            if SLOTS - 4 <= done < SLOTS - 2:
                add_last(done, nc.gpsimd)
            for g, r, qk in tables.get(slot, []):
                table_coef(g, r, qk, nc.gpsimd)
            if 0 <= done < SLOTS and done % 2 == 1:
                store(done // 4, (done % 4) // 2)
            if slot in values_at and values_at[slot] % 2 == 1:
                store(values_at[slot] // 2, 2)
